import numpy as np
import ml_dtypes


def mxq(x, axis, fmt="e4m3"):
    dtype, down = {"e4m3": (ml_dtypes.float8_e4m3fn, 7), "e5m2": (ml_dtypes.float8_e5m2, 14)}[fmt]
    v = np.moveaxis(np.asarray(x, np.float32).astype(ml_dtypes.bfloat16).astype(np.float64), axis, -1)
    blocks = v.reshape(v.shape[:-1] + (-1, 32))
    amax = np.abs(blocks).max(-1, keepdims=True)
    byte = np.maximum(np.where(amax > 0, np.frexp(amax)[1] - 1 + 127, 0) - down, 1)
    scale = np.exp2(byte - 127.0)
    codes = (blocks / scale).astype(np.float32).astype(dtype).astype(np.float64)
    return np.moveaxis((codes * scale).reshape(v.shape), -1, axis)


WIDE = False


def mx_kscale(k):
    if not WIDE:
        return np.ones(k)
    levels = np.array([10, -10, 5, -5, 0])
    a = np.random.permutation(np.resize(levels, k // 512 * 4)).reshape(k // 512, 4)
    idx = np.arange(k)
    return np.exp2(a[idx // 512, idx % 128 // 32])


BF16 = ml_dtypes.bfloat16


def bf(x):
    return np.asarray(x, np.float32).astype(BF16)


def f64(x):
    return np.asarray(x).astype(np.float64)


B, N, D, DK, DV, HQ, WQ, HS, WS = 2, 16, 1024, 512, 128, 8, 8, 4, 4
U = HQ * WQ
V = HS * WS
VS = 4.0 * np.sqrt(N) / U


def setup_inputs():
    s = mx_kscale(D)
    sc = s[None, :, None, None]
    offset = np.random.standard_normal((B, D))[:, :, None, None]
    return {"query": bf((np.random.standard_normal((B, D, HQ, WQ)) + offset) * sc),
            "support": bf(np.random.standard_normal((N, D, HS, WS)) * sc),
            "Wk": bf(np.random.standard_normal((DK, D)) / np.sqrt(D) / s[None, :]),
            "Wv": bf(np.random.standard_normal((DV, D)) * VS / np.sqrt(D) / s[None, :])}


def reference(query, support, Wk, Wv):
    qf = mxq(f64(query).reshape(B, D, U), 1, "e4m3")
    sf = mxq(f64(support).reshape(N, D, V), 1, "e4m3")
    wk = mxq(f64(Wk), 1, "e4m3")
    wv = mxq(f64(Wv), 1, "e4m3")
    q = wk @ qf
    support_key = wk @ sf
    support_value = wv @ sf
    scores = (mxq(q, 1, "e4m3").transpose(0, 2, 1)[:, None] @ mxq(support_key, 1, "e4m3")[None]) / np.sqrt(DK)
    e = np.exp(scores - scores.max(1, keepdims=True))
    attn = e / e.sum(1, keepdims=True)
    return (attn.sum(2)[:, :, None, :] * support_value[None]).sum(1)

@@ -1,0 +1,222 @@
+import math
+from contextlib import ExitStack
+
+import concourse.mybir as mybir
+from concourse.masks import make_identity
+
+F32 = mybir.dt.float32
+BF16 = mybir.dt.bfloat16
+U32 = mybir.dt.uint32
+U8 = mybir.dt.uint8
+FP8X4 = mybir.dt.float8_e4m3fn_x4
+ALU = mybir.AluOpType
+FUNC = mybir.ActivationFunctionType
+AXIS = mybir.AxisListType
+
+P = 128
+PACK = 4
+K_PASS = P * PACK
+
+B, N_SUP, D, DK, DV = 2, 16, 1024, 512, 128
+U = 64
+V = 16
+D_PASSES = D // K_PASS
+KEY_CHUNKS = DK // P
+VAL_CHUNK = KEY_CHUNKS
+SUP_BLOCKS = N_SUP * V // P
+QUERY_BLOCK = SUP_BLOCKS
+IMAGES_PER_SUP_BLOCK = N_SUP // SUP_BLOCKS
+
+FLOPS = 2 * D * (DK * (B * U + N_SUP * V) + DV * N_SUP * V) + 2 * DK * B * U * N_SUP * V
+
+
+def pass_cols(c):
+    return slice(c * P, (c + 1) * P)
+
+
+def tile_crossattention_pa_s_kernel(tc, query, support, Wk, Wv, out):
+    nc = tc.nc
+    with ExitStack() as ctx:
+        const = ctx.enter_context(tc.tile_pool(name="const", bufs=1))
+        keep = ctx.enter_context(tc.tile_pool(name="keep", bufs=1))
+        raws = ctx.enter_context(tc.tile_pool(name="raws", bufs=(SUP_BLOCKS + 1) * D_PASSES))
+        stage = ctx.enter_context(tc.tile_pool(name="stage", bufs=3))
+        flip_psum = ctx.enter_context(tc.psum_pool(name="flip_psum", bufs=3))
+        proj_psum = ctx.enter_context(tc.psum_pool(name="proj_psum", bufs=3))
+        tail_psum = ctx.enter_context(tc.psum_pool(name="tail_psum", bufs=1))
+
+        w_rows = keep.tile([P, KEY_CHUNKS + 1, D], BF16)
+        wk_view = Wk.rearrange("(p t) d -> p t d", t=KEY_CHUNKS)
+        half = KEY_CHUNKS // 2
+        nc.sync.dma_start(out=w_rows[:, 0:half, :], in_=wk_view[:, 0:half, :])
+        nc.sync.dma_start(out=w_rows[:, half:KEY_CHUNKS, :], in_=wk_view[:, half:KEY_CHUNKS, :])
+
+        block_images = [
+            support[h * IMAGES_PER_SUP_BLOCK : (h + 1) * IMAGES_PER_SUP_BLOCK] for h in range(SUP_BLOCKS)
+        ] + [query]
+        raw_pieces = {}
+        for blk, images in enumerate(block_images):
+            for c in range(D_PASSES):
+                raw = raws.tile([P, K_PASS], BF16)
+                nc.sync.dma_start(
+                    out=raw[:].rearrange("p (i f) -> p i f", i=images.shape[0]),
+                    in_=images[:, c * K_PASS : (c + 1) * K_PASS].rearrange("i (p j) h w -> p i (j h w)", j=PACK),
+                )
+                raw_pieces[(blk, c)] = raw
+        nc.sync.dma_start(out=w_rows[:, VAL_CHUNK, :], in_=Wv)
+
+        ident = const.tile([P, P], F32)
+        make_identity(nc, ident[:])
+        same_pos = const.tile([P, V], F32)
+        nc.vector.tensor_reduce(
+            out=same_pos[:], in_=ident[:].rearrange("p (i v) -> p v i", v=V), axis=AXIS.X, op=ALU.add
+        )
+        inv_sum = const.tile([P, B, V], F32)
+        nc.vector.memset(inv_sum[:], 0.0)
+        zero_col = const.tile([P, 1], F32)
+        one_col = const.tile([P, 1], F32)
+        nc.vector.memset(zero_col[:], 0.0)
+        nc.scalar.activation(out=one_col[:], in_=zero_col[:], func=FUNC.Exp)
+
+        w_codes = keep.tile([P, KEY_CHUNKS + 1, D_PASSES * P], U32, align_bytes=64)
+        w_scales = keep.tile([P, KEY_CHUNKS + 1, D_PASSES * P], U8, align_bytes=64)
+        x_codes = keep.tile([P, SUP_BLOCKS + 1, D_PASSES * P], U32, align_bytes=64)
+        x_scales = keep.tile([P, SUP_BLOCKS + 1, D_PASSES * P], U8, align_bytes=64)
+        proj_codes = keep.tile([P, (SUP_BLOCKS + 1) * P], U32, align_bytes=64)
+        proj_scales = keep.tile([P, (SUP_BLOCKS + 1) * P], U8, align_bytes=64)
+
+        def quantise_weight_chunk(t):
+            words = w_rows[:, t, :].bitcast(F32).rearrange("p (c q u) -> p c u q", c=D_PASSES, u=2)
+            flipped = flip_psum.tile([P, D_PASSES, 2, P], F32)
+            for c in range(D_PASSES):
+                for u in range(2):
+                    nc.tensor.transpose(flipped[:, c, u, :], words[:, c, u, :], ident[:])
+            w_grouped = stage.tile([P, D_PASSES * P * PACK], BF16, align_bytes=64)
+            nc.scalar.copy(
+                out=w_grouped[:].bitcast(F32).rearrange("p (c r u) -> p c r u", c=D_PASSES, u=2),
+                in_=flipped[:].rearrange("p c u r -> p c r u"),
+            )
+            nc.vector.quantize_mx(out=w_codes[:, t, :].bitcast(FP8X4), scales=w_scales[:, t, :], in_=w_grouped[:])
+
+        def quantise_piece(blk, c):
+            n_images = block_images[blk].shape[0]
+            x_grouped = stage.tile([P, K_PASS], BF16, align_bytes=64)
+            nc.vector.tensor_copy(
+                out=x_grouped[:].rearrange("p (i s j) -> p i s j", i=n_images, j=PACK),
+                in_=raw_pieces[(blk, c)][:].rearrange("p (i j s) -> p i s j", i=n_images, j=PACK),
+            )
+            nc.vector.quantize_mx(
+                out=x_codes[:, blk, pass_cols(c)].bitcast(FP8X4),
+                scales=x_scales[:, blk, pass_cols(c)],
+                in_=x_grouped[:],
+            )
+
+        def project_with_wk(blk):
+            proj = proj_psum.tile([P, KEY_CHUNKS, P], F32)
+            for t in range(KEY_CHUNKS):
+                for c in range(D_PASSES):
+                    nc.tensor.matmul_mx(
+                        out=proj[:, t, :],
+                        lhsT=w_codes[:, t, pass_cols(c)].bitcast(FP8X4),
+                        lhsT_scale=w_scales[:, t, pass_cols(c)],
+                        rhs=x_codes[:, blk, pass_cols(c)].bitcast(FP8X4),
+                        rhs_scale=x_scales[:, blk, pass_cols(c)],
+                        start=(c == 0),
+                        stop=(c == D_PASSES - 1),
+                    )
+            proj_grouped = stage.tile([P, P * PACK], BF16, align_bytes=64)
+            nc.scalar.copy(
+                out=proj_grouped[:].rearrange("p (w t) -> p w t", t=PACK), in_=proj[:].rearrange("p t w -> p w t")
+            )
+            nc.vector.quantize_mx(
+                out=proj_codes[:, blk * P : (blk + 1) * P].bitcast(FP8X4),
+                scales=proj_scales[:, blk * P : (blk + 1) * P],
+                in_=proj_grouped[:],
+            )
+
+        for t in range(KEY_CHUNKS):
+            quantise_weight_chunk(t)
+        for blk in range(SUP_BLOCKS + 1):
+            for c in range(D_PASSES):
+                quantise_piece(blk, c)
+            project_with_wk(blk)
+
+        quantise_weight_chunk(VAL_CHUNK)
+        val_ps = tail_psum.tile([P, SUP_BLOCKS, DV], F32)
+        for h in range(SUP_BLOCKS):
+            for c in range(D_PASSES):
+                nc.tensor.matmul_mx(
+                    out=val_ps[:, h, :],
+                    lhsT=x_codes[:, h, pass_cols(c)].bitcast(FP8X4),
+                    lhsT_scale=x_scales[:, h, pass_cols(c)],
+                    rhs=w_codes[:, VAL_CHUNK, pass_cols(c)].bitcast(FP8X4),
+                    rhs_scale=w_scales[:, VAL_CHUNK, pass_cols(c)],
+                    start=(c == 0),
+                    stop=(c == D_PASSES - 1),
+                )
+        val_t = keep.tile([P, SUP_BLOCKS, DV], F32)
+        nc.scalar.copy(out=val_t[:], in_=val_ps[:])
+
+        key_cols = slice(0, SUP_BLOCKS * P)
+        query_cols = slice(QUERY_BLOCK * P, (QUERY_BLOCK + 1) * P)
+        scores = tail_psum.tile([P, N_SUP * V], F32, tag="chain")
+        nc.tensor.matmul_mx(
+            out=scores[:],
+            lhsT=proj_codes[:, query_cols].bitcast(FP8X4),
+            lhsT_scale=proj_scales[:, query_cols],
+            rhs=proj_codes[:, key_cols].bitcast(FP8X4),
+            rhs_scale=proj_scales[:, key_cols],
+            start=True,
+            stop=True,
+        )
+
+        top = keep.tile([P, V], F32)
+        nc.vector.tensor_reduce(
+            out=top[:], in_=scores[:].rearrange("p (n v) -> p v n", v=V), axis=AXIS.X, op=ALU.max
+        )
+        shifted = keep.tile([P, N_SUP * V], F32)
+        nc.vector.tensor_tensor(
+            out=shifted[:].rearrange("p (n v) -> p n v", v=V),
+            in0=scores[:].rearrange("p (n v) -> p n v", v=V),
+            in1=top[:].unsqueeze(1).to_broadcast([P, N_SUP, V]),
+            op=ALU.subtract,
+        )
+        expd = keep.tile([P, N_SUP * V], F32)
+        nc.scalar.activation(out=expd[:], in_=shifted[:], func=FUNC.Exp, scale=1.0 / math.sqrt(DK))
+        sums = keep.tile([P, V], F32)
+        nc.vector.tensor_reduce(
+            out=sums[:], in_=expd[:].rearrange("p (n v) -> p v n", v=V), axis=AXIS.X, op=ALU.add
+        )
+        for b in range(B):
+            own = slice(b * U, (b + 1) * U)
+            nc.vector.reciprocal(out=inv_sum[own, b, :], in_=sums[own, :])
+
+        crossed = tail_psum.tile([P, SUP_BLOCKS, B * V], F32, tag="chain")
+        for h in range(SUP_BLOCKS):
+            nc.tensor.matmul(
+                out=crossed[:, h, :],
+                lhsT=expd[:, h * P : (h + 1) * P],
+                rhs=inv_sum[:].rearrange("p b v -> p (b v)"),
+                start=True,
+                stop=True,
+            )
+        weight = keep.tile([P, SUP_BLOCKS, B * V], F32)
+        nc.vector.tensor_tensor(
+            out=weight[:].rearrange("p h (b v) -> p (h b) v", v=V),
+            in0=crossed[:].rearrange("p h (b v) -> p (h b) v", v=V),
+            in1=same_pos[:].unsqueeze(1).to_broadcast([P, SUP_BLOCKS * B, V]),
+            op=ALU.mult,
+        )
+
+        result_ps = tail_psum.tile([P, B * V], F32, tag="chain")
+        for h in range(SUP_BLOCKS):
+            nc.tensor.matmul(
+                out=result_ps[:],
+                lhsT=val_t[:, h, :],
+                rhs=weight[:, h, :],
+                start=(h == 0),
+                stop=(h == SUP_BLOCKS - 1),
+            )
+        result = keep.tile([P, B, V], F32)
+        nc.vector.tensor_copy(out=result[:].rearrange("p b v -> p (b v)"), in_=result_ps[:])
+        nc.sync.dma_start(out=out.rearrange("b c v -> c b v"), in_=result[:])

@@ -24,7 +24,7 @@ D_PASSES = D // K_PASS
 KEY_CHUNKS = DK // P
 VAL_CHUNK = KEY_CHUNKS
 SUP_BLOCKS = N_SUP * V // P
-QUERY_BLOCK = SUP_BLOCKS
+BLOCKS = 1 + SUP_BLOCKS
 IMAGES_PER_SUP_BLOCK = N_SUP // SUP_BLOCKS
 
 FLOPS = 2 * D * (DK * (B * U + N_SUP * V) + DV * N_SUP * V) + 2 * DK * B * U * N_SUP * V
@@ -34,12 +34,17 @@ def pass_cols(c):
     return slice(c * P, (c + 1) * P)
 
 
+def block_cols(blk):
+    return slice(blk * P, (blk + 1) * P)
+
+
 def tile_crossattention_pa_s_kernel(tc, query, support, Wk, Wv, out):
     nc = tc.nc
     with ExitStack() as ctx:
+        ctx.enter_context(tc.manual_schedule())
         const = ctx.enter_context(tc.tile_pool(name="const", bufs=1))
         keep = ctx.enter_context(tc.tile_pool(name="keep", bufs=1))
-        raws = ctx.enter_context(tc.tile_pool(name="raws", bufs=(SUP_BLOCKS + 1) * D_PASSES))
+        raws = ctx.enter_context(tc.tile_pool(name="raws", bufs=BLOCKS * D_PASSES))
         stage = ctx.enter_context(tc.tile_pool(name="stage", bufs=3))
         flip_psum = ctx.enter_context(tc.psum_pool(name="flip_psum", bufs=3))
         proj_psum = ctx.enter_context(tc.psum_pool(name="proj_psum", bufs=3))
@@ -51,9 +56,9 @@ def tile_crossattention_pa_s_kernel(tc, query, support, Wk, Wv, out):
         nc.sync.dma_start(out=w_rows[:, 0:half, :], in_=wk_view[:, 0:half, :])
         nc.sync.dma_start(out=w_rows[:, half:KEY_CHUNKS, :], in_=wk_view[:, half:KEY_CHUNKS, :])
 
-        block_images = [
+        block_images = [query] + [
             support[h * IMAGES_PER_SUP_BLOCK : (h + 1) * IMAGES_PER_SUP_BLOCK] for h in range(SUP_BLOCKS)
-        ] + [query]
+        ]
         raw_pieces = {}
         for blk, images in enumerate(block_images):
             for c in range(D_PASSES):
@@ -80,12 +85,12 @@ def tile_crossattention_pa_s_kernel(tc, query, support, Wk, Wv, out):
 
         w_codes = keep.tile([P, KEY_CHUNKS + 1, D_PASSES * P], U32, align_bytes=64)
         w_scales = keep.tile([P, KEY_CHUNKS + 1, D_PASSES * P], U8, align_bytes=64)
-        x_codes = keep.tile([P, SUP_BLOCKS + 1, D_PASSES * P], U32, align_bytes=64)
-        x_scales = keep.tile([P, SUP_BLOCKS + 1, D_PASSES * P], U8, align_bytes=64)
-        proj_codes = keep.tile([P, (SUP_BLOCKS + 1) * P], U32, align_bytes=64)
-        proj_scales = keep.tile([P, (SUP_BLOCKS + 1) * P], U8, align_bytes=64)
+        x_codes = keep.tile([P, BLOCKS, D_PASSES * P], U32, align_bytes=64)
+        x_scales = keep.tile([P, BLOCKS, D_PASSES * P], U8, align_bytes=64)
+        proj_codes = keep.tile([P, BLOCKS * P], U32, align_bytes=64)
+        proj_scales = keep.tile([P, BLOCKS * P], U8, align_bytes=64)
 
-        def quantise_weight_chunk(t):
+        def flip_weight_chunk(t):
             words = w_rows[:, t, :].bitcast(F32).rearrange("p (c q u) -> p c u q", c=D_PASSES, u=2)
             flipped = flip_psum.tile([P, D_PASSES, 2, P], F32)
             for c in range(D_PASSES):
@@ -96,6 +101,9 @@ def tile_crossattention_pa_s_kernel(tc, query, support, Wk, Wv, out):
                 out=w_grouped[:].bitcast(F32).rearrange("p (c r u) -> p c r u", c=D_PASSES, u=2),
                 in_=flipped[:].rearrange("p c u r -> p c r u"),
             )
+            return w_grouped
+
+        def quantise_weight_chunk(t, w_grouped):
             nc.vector.quantize_mx(out=w_codes[:, t, :].bitcast(FP8X4), scales=w_scales[:, t, :], in_=w_grouped[:])
 
         def quantise_piece(blk, c):
@@ -129,41 +137,26 @@ def tile_crossattention_pa_s_kernel(tc, query, support, Wk, Wv, out):
                 out=proj_grouped[:].rearrange("p (w t) -> p w t", t=PACK), in_=proj[:].rearrange("p t w -> p w t")
             )
             nc.vector.quantize_mx(
-                out=proj_codes[:, blk * P : (blk + 1) * P].bitcast(FP8X4),
-                scales=proj_scales[:, blk * P : (blk + 1) * P],
+                out=proj_codes[:, block_cols(blk)].bitcast(FP8X4),
+                scales=proj_scales[:, block_cols(blk)],
                 in_=proj_grouped[:],
             )
 
         for t in range(KEY_CHUNKS):
-            quantise_weight_chunk(t)
-        for blk in range(SUP_BLOCKS + 1):
+            quantise_weight_chunk(t, flip_weight_chunk(t))
+        for blk in range(BLOCKS):
             for c in range(D_PASSES):
                 quantise_piece(blk, c)
             project_with_wk(blk)
 
-        quantise_weight_chunk(VAL_CHUNK)
-        val_ps = tail_psum.tile([P, SUP_BLOCKS, DV], F32)
-        for h in range(SUP_BLOCKS):
-            for c in range(D_PASSES):
-                nc.tensor.matmul_mx(
-                    out=val_ps[:, h, :],
-                    lhsT=x_codes[:, h, pass_cols(c)].bitcast(FP8X4),
-                    lhsT_scale=x_scales[:, h, pass_cols(c)],
-                    rhs=w_codes[:, VAL_CHUNK, pass_cols(c)].bitcast(FP8X4),
-                    rhs_scale=w_scales[:, VAL_CHUNK, pass_cols(c)],
-                    start=(c == 0),
-                    stop=(c == D_PASSES - 1),
-                )
-        val_t = keep.tile([P, SUP_BLOCKS, DV], F32)
-        nc.scalar.copy(out=val_t[:], in_=val_ps[:])
+        wv_grouped = flip_weight_chunk(VAL_CHUNK)
 
-        key_cols = slice(0, SUP_BLOCKS * P)
-        query_cols = slice(QUERY_BLOCK * P, (QUERY_BLOCK + 1) * P)
+        key_cols = slice(P, BLOCKS * P)
         scores = tail_psum.tile([P, N_SUP * V], F32, tag="chain")
         nc.tensor.matmul_mx(
             out=scores[:],
-            lhsT=proj_codes[:, query_cols].bitcast(FP8X4),
-            lhsT_scale=proj_scales[:, query_cols],
+            lhsT=proj_codes[:, block_cols(0)].bitcast(FP8X4),
+            lhsT_scale=proj_scales[:, block_cols(0)],
             rhs=proj_codes[:, key_cols].bitcast(FP8X4),
             rhs_scale=proj_scales[:, key_cols],
             start=True,
@@ -183,6 +176,23 @@ def tile_crossattention_pa_s_kernel(tc, query, support, Wk, Wv, out):
         )
         expd = keep.tile([P, N_SUP * V], F32)
         nc.scalar.activation(out=expd[:], in_=shifted[:], func=FUNC.Exp, scale=1.0 / math.sqrt(DK))
+
+        quantise_weight_chunk(VAL_CHUNK, wv_grouped)
+        val_ps = tail_psum.tile([P, SUP_BLOCKS, DV], F32)
+        for h in range(SUP_BLOCKS):
+            for c in range(D_PASSES):
+                nc.tensor.matmul_mx(
+                    out=val_ps[:, h, :],
+                    lhsT=x_codes[:, 1 + h, pass_cols(c)].bitcast(FP8X4),
+                    lhsT_scale=x_scales[:, 1 + h, pass_cols(c)],
+                    rhs=w_codes[:, VAL_CHUNK, pass_cols(c)].bitcast(FP8X4),
+                    rhs_scale=w_scales[:, VAL_CHUNK, pass_cols(c)],
+                    start=(c == 0),
+                    stop=(c == D_PASSES - 1),
+                )
+        val_t = keep.tile([P, SUP_BLOCKS, DV], F32)
+        nc.scalar.copy(out=val_t[:], in_=val_ps[:])
+
         sums = keep.tile([P, V], F32)
         nc.vector.tensor_reduce(
             out=sums[:], in_=expd[:].rearrange("p (n v) -> p v n", v=V), axis=AXIS.X, op=ALU.add

@@ -8,6 +8,7 @@ F32 = mybir.dt.float32
 BF16 = mybir.dt.bfloat16
 U32 = mybir.dt.uint32
 U8 = mybir.dt.uint8
+I32 = mybir.dt.int32
 FP8X4 = mybir.dt.float8_e4m3fn_x4
 ALU = mybir.AluOpType
 FUNC = mybir.ActivationFunctionType
@@ -26,6 +27,8 @@ VAL_CHUNK = KEY_CHUNKS
 SUP_BLOCKS = N_SUP * V // P
 BLOCKS = 1 + SUP_BLOCKS
 IMAGES_PER_SUP_BLOCK = N_SUP // SUP_BLOCKS
+PARTS = [(blk, 0, D_PASSES) for blk in range(BLOCKS - 1)] + [(BLOCKS - 1, c, 1) for c in range(D_PASSES)]
+IDLE_PASSES = 2
 
 FLOPS = 2 * D * (DK * (B * U + N_SUP * V) + DV * N_SUP * V) + 2 * DK * B * U * N_SUP * V
 
@@ -44,10 +47,10 @@ def tile_crossattention_pa_s_kernel(tc, query, support, Wk, Wv, out):
         ctx.enter_context(tc.manual_schedule())
         const = ctx.enter_context(tc.tile_pool(name="const", bufs=1))
         keep = ctx.enter_context(tc.tile_pool(name="keep", bufs=1))
-        raws = ctx.enter_context(tc.tile_pool(name="raws", bufs=BLOCKS * D_PASSES))
+        raws = ctx.enter_context(tc.tile_pool(name="raws", bufs=len(PARTS)))
         stage = ctx.enter_context(tc.tile_pool(name="stage", bufs=3))
-        flip_psum = ctx.enter_context(tc.psum_pool(name="flip_psum", bufs=3))
-        proj_psum = ctx.enter_context(tc.psum_pool(name="proj_psum", bufs=3))
+        flip_psum = ctx.enter_context(tc.psum_pool(name="flip_psum", bufs=2))
+        proj_psum = ctx.enter_context(tc.psum_pool(name="proj_psum", bufs=BLOCKS))
         tail_psum = ctx.enter_context(tc.psum_pool(name="tail_psum", bufs=1))
 
         w_rows = keep.tile([P, KEY_CHUNKS + 1, D], BF16)
@@ -59,19 +62,39 @@ def tile_crossattention_pa_s_kernel(tc, query, support, Wk, Wv, out):
         block_images = [query] + [
             support[h * IMAGES_PER_SUP_BLOCK : (h + 1) * IMAGES_PER_SUP_BLOCK] for h in range(SUP_BLOCKS)
         ]
-        raw_pieces = {}
-        for blk, images in enumerate(block_images):
-            for c in range(D_PASSES):
-                raw = raws.tile([P, K_PASS], BF16)
-                nc.sync.dma_start(
-                    out=raw[:].rearrange("p (i f) -> p i f", i=images.shape[0]),
-                    in_=images[:, c * K_PASS : (c + 1) * K_PASS].rearrange("i (p j) h w -> p i (j h w)", j=PACK),
-                )
-                raw_pieces[(blk, c)] = raw
+        raw_parts = []
+        for blk, first_pass, n_passes in PARTS:
+            images = block_images[blk]
+            channels = slice(first_pass * K_PASS, (first_pass + n_passes) * K_PASS)
+            raw = raws.tile([P, n_passes * K_PASS], BF16)
+            nc.sync.dma_start(
+                out=raw[:].rearrange("p (i c f) -> p i c f", i=images.shape[0], c=n_passes),
+                in_=images[:, channels].rearrange("i (c p j) h w -> p i c (j h w)", c=n_passes, j=PACK),
+            )
+            raw_parts.append(raw)
         nc.sync.dma_start(out=w_rows[:, VAL_CHUNK, :], in_=Wv)
 
         ident = const.tile([P, P], F32)
         make_identity(nc, ident[:])
+        zeros = const.tile([P, K_PASS * PACK], BF16, align_bytes=64)
+        idle_codes = const.tile([P, K_PASS], U32, align_bytes=64)
+        idle_scales = const.tile([P, K_PASS], U8, align_bytes=64)
+        nc.vector.memset(zeros[:].bitcast(I32), 0)
+        nc.vector.quantize_mx(out=idle_codes[:].bitcast(FP8X4), scales=idle_scales[:], in_=zeros[:])
+        idle_ps = tail_psum.tile([P, K_PASS], F32)
+
+        def hold_clock():
+            for i in range(IDLE_PASSES):
+                nc.tensor.matmul_mx(
+                    out=idle_ps[:],
+                    lhsT=idle_codes[:, 0:P].bitcast(FP8X4),
+                    lhsT_scale=idle_scales[:, 0:P],
+                    rhs=idle_codes[:].bitcast(FP8X4),
+                    rhs_scale=idle_scales[:],
+                    start=True,
+                    stop=True,
+                )
+
         same_pos = const.tile([P, V], F32)
         nc.vector.tensor_reduce(
             out=same_pos[:], in_=ident[:].rearrange("p (i v) -> p v i", v=V), axis=AXIS.X, op=ALU.add
@@ -106,17 +129,17 @@ def tile_crossattention_pa_s_kernel(tc, query, support, Wk, Wv, out):
         def quantise_weight_chunk(t, w_grouped):
             nc.vector.quantize_mx(out=w_codes[:, t, :].bitcast(FP8X4), scales=w_scales[:, t, :], in_=w_grouped[:])
 
-        def quantise_piece(blk, c):
+        def quantise_part(part):
+            blk, first_pass, n_passes = PARTS[part]
             n_images = block_images[blk].shape[0]
-            x_grouped = stage.tile([P, K_PASS], BF16, align_bytes=64)
+            x_grouped = stage.tile([P, n_passes * K_PASS], BF16, align_bytes=64, tag="x_grouped")
             nc.vector.tensor_copy(
-                out=x_grouped[:].rearrange("p (i s j) -> p i s j", i=n_images, j=PACK),
-                in_=raw_pieces[(blk, c)][:].rearrange("p (i j s) -> p i s j", i=n_images, j=PACK),
+                out=x_grouped[:].rearrange("p (c i s j) -> p c i s j", c=n_passes, i=n_images, j=PACK),
+                in_=raw_parts[part][:].rearrange("p (i c j s) -> p c i s j", c=n_passes, i=n_images, j=PACK),
             )
+            cols = slice(first_pass * P, (first_pass + n_passes) * P)
             nc.vector.quantize_mx(
-                out=x_codes[:, blk, pass_cols(c)].bitcast(FP8X4),
-                scales=x_scales[:, blk, pass_cols(c)],
-                in_=x_grouped[:],
+                out=x_codes[:, blk, cols].bitcast(FP8X4), scales=x_scales[:, blk, cols], in_=x_grouped[:]
             )
 
         def project_with_wk(blk):
@@ -136,18 +159,25 @@ def tile_crossattention_pa_s_kernel(tc, query, support, Wk, Wv, out):
             nc.scalar.copy(
                 out=proj_grouped[:].rearrange("p (w t) -> p w t", t=PACK), in_=proj[:].rearrange("p t w -> p w t")
             )
+            return proj_grouped
+
+        def quantise_projection(blk, proj_grouped):
             nc.vector.quantize_mx(
                 out=proj_codes[:, block_cols(blk)].bitcast(FP8X4),
                 scales=proj_scales[:, block_cols(blk)],
                 in_=proj_grouped[:],
             )
 
-        for t in range(KEY_CHUNKS):
+        for t in range(0, half):
             quantise_weight_chunk(t, flip_weight_chunk(t))
+        quantise_part(0)
+        for t in range(half, KEY_CHUNKS):
+            quantise_weight_chunk(t, flip_weight_chunk(t))
+        hold_clock()
+        for part in range(1, len(PARTS)):
+            quantise_part(part)
         for blk in range(BLOCKS):
-            for c in range(D_PASSES):
-                quantise_piece(blk, c)
-            project_with_wk(blk)
+            quantise_projection(blk, project_with_wk(blk))
 
         wv_grouped = flip_weight_chunk(VAL_CHUNK)
 
@@ -162,6 +192,7 @@ def tile_crossattention_pa_s_kernel(tc, query, support, Wk, Wv, out):
             start=True,
             stop=True,
         )
+        hold_clock()
 
         top = keep.tile([P, V], F32)
         nc.vector.tensor_reduce(
@@ -190,6 +221,7 @@ def tile_crossattention_pa_s_kernel(tc, query, support, Wk, Wv, out):
                     start=(c == 0),
                     stop=(c == D_PASSES - 1),
                 )
+        hold_clock()
         val_t = keep.tile([P, SUP_BLOCKS, DV], F32)
         nc.scalar.copy(out=val_t[:], in_=val_ps[:])
 
@@ -201,29 +233,28 @@ def tile_crossattention_pa_s_kernel(tc, query, support, Wk, Wv, out):
             own = slice(b * U, (b + 1) * U)
             nc.vector.reciprocal(out=inv_sum[own, b, :], in_=sums[own, :])
 
-        crossed = tail_psum.tile([P, SUP_BLOCKS, B * V], F32, tag="chain")
+        weights = []
         for h in range(SUP_BLOCKS):
+            crossed = flip_psum.tile([P, B, V], F32, tag="flipped")
             nc.tensor.matmul(
-                out=crossed[:, h, :],
+                out=crossed[:].rearrange("p b v -> p (b v)"),
                 lhsT=expd[:, h * P : (h + 1) * P],
                 rhs=inv_sum[:].rearrange("p b v -> p (b v)"),
                 start=True,
                 stop=True,
             )
-        weight = keep.tile([P, SUP_BLOCKS, B * V], F32)
-        nc.vector.tensor_tensor(
-            out=weight[:].rearrange("p h (b v) -> p (h b) v", v=V),
-            in0=crossed[:].rearrange("p h (b v) -> p (h b) v", v=V),
-            in1=same_pos[:].unsqueeze(1).to_broadcast([P, SUP_BLOCKS * B, V]),
-            op=ALU.mult,
-        )
+            weight = keep.tile([P, B, V], F32, name="weight%d" % h)
+            nc.vector.tensor_tensor(
+                out=weight[:], in0=crossed[:], in1=same_pos[:].unsqueeze(1).to_broadcast([P, B, V]), op=ALU.mult
+            )
+            weights.append(weight)
 
         result_ps = tail_psum.tile([P, B * V], F32, tag="chain")
         for h in range(SUP_BLOCKS):
             nc.tensor.matmul(
                 out=result_ps[:],
                 lhsT=val_t[:, h, :],
-                rhs=weight[:, h, :],
+                rhs=weights[h][:].rearrange("p b v -> p (b v)"),
                 start=(h == 0),
                 stop=(h == SUP_BLOCKS - 1),
             )

@@ -28,7 +28,8 @@ SUP_BLOCKS = N_SUP * V // P
 BLOCKS = 1 + SUP_BLOCKS
 IMAGES_PER_SUP_BLOCK = N_SUP // SUP_BLOCKS
 PARTS = [(blk, 0, D_PASSES) for blk in range(BLOCKS - 1)] + [(BLOCKS - 1, c, 1) for c in range(D_PASSES)]
-IDLE_PASSES = 2
+HOLD_PASSES = 2
+START_PASSES = 4
 
 FLOPS = 2 * D * (DK * (B * U + N_SUP * V) + DV * N_SUP * V) + 2 * DK * B * U * N_SUP * V
 
@@ -56,8 +57,8 @@ def tile_crossattention_pa_s_kernel(tc, query, support, Wk, Wv, out):
         w_rows = keep.tile([P, KEY_CHUNKS + 1, D], BF16)
         wk_view = Wk.rearrange("(p t) d -> p t d", t=KEY_CHUNKS)
         half = KEY_CHUNKS // 2
-        nc.sync.dma_start(out=w_rows[:, 0:half, :], in_=wk_view[:, 0:half, :])
-        nc.sync.dma_start(out=w_rows[:, half:KEY_CHUNKS, :], in_=wk_view[:, half:KEY_CHUNKS, :])
+        for t in range(KEY_CHUNKS):
+            nc.sync.dma_start(out=w_rows[:, t, :], in_=wk_view[:, t, :])
 
         block_images = [query] + [
             support[h * IMAGES_PER_SUP_BLOCK : (h + 1) * IMAGES_PER_SUP_BLOCK] for h in range(SUP_BLOCKS)
@@ -83,8 +84,8 @@ def tile_crossattention_pa_s_kernel(tc, query, support, Wk, Wv, out):
         nc.vector.quantize_mx(out=idle_codes[:].bitcast(FP8X4), scales=idle_scales[:], in_=zeros[:])
         idle_ps = tail_psum.tile([P, K_PASS], F32)
 
-        def hold_clock():
-            for i in range(IDLE_PASSES):
+        def hold_clock(n_passes):
+            for i in range(n_passes):
                 nc.tensor.matmul_mx(
                     out=idle_ps[:],
                     lhsT=idle_codes[:, 0:P].bitcast(FP8X4),
@@ -129,14 +130,18 @@ def tile_crossattention_pa_s_kernel(tc, query, support, Wk, Wv, out):
         def quantise_weight_chunk(t, w_grouped):
             nc.vector.quantize_mx(out=w_codes[:, t, :].bitcast(FP8X4), scales=w_scales[:, t, :], in_=w_grouped[:])
 
-        def quantise_part(part):
+        def regroup_part(part, copy):
             blk, first_pass, n_passes = PARTS[part]
             n_images = block_images[blk].shape[0]
             x_grouped = stage.tile([P, n_passes * K_PASS], BF16, align_bytes=64, tag="x_grouped")
-            nc.vector.tensor_copy(
-                out=x_grouped[:].rearrange("p (c i s j) -> p c i s j", c=n_passes, i=n_images, j=PACK),
-                in_=raw_parts[part][:].rearrange("p (i c j s) -> p c i s j", c=n_passes, i=n_images, j=PACK),
-            )
+            grouped_view = x_grouped[:].rearrange("p (c i s j) -> p c i s j", c=n_passes, i=n_images, j=PACK)
+            raw_view = raw_parts[part][:].rearrange("p (i c j s) -> p c i s j", c=n_passes, i=n_images, j=PACK)
+            for c in range(n_passes):
+                copy(out=grouped_view[:, c], in_=raw_view[:, c])
+            return x_grouped
+
+        def quantise_part(part, x_grouped):
+            blk, first_pass, n_passes = PARTS[part]
             cols = slice(first_pass * P, (first_pass + n_passes) * P)
             nc.vector.quantize_mx(
                 out=x_codes[:, blk, cols].bitcast(FP8X4), scales=x_scales[:, blk, cols], in_=x_grouped[:]
@@ -170,12 +175,14 @@ def tile_crossattention_pa_s_kernel(tc, query, support, Wk, Wv, out):
 
         for t in range(0, half):
             quantise_weight_chunk(t, flip_weight_chunk(t))
-        quantise_part(0)
+        quantise_part(0, regroup_part(0, nc.vector.tensor_copy))
         for t in range(half, KEY_CHUNKS):
             quantise_weight_chunk(t, flip_weight_chunk(t))
-        hold_clock()
-        for part in range(1, len(PARTS)):
-            quantise_part(part)
+        hold_clock(START_PASSES)
+        whole_block = regroup_part(1, nc.scalar.copy)
+        quantise_part(2, regroup_part(2, nc.vector.tensor_copy))
+        quantise_part(1, whole_block)
+        quantise_part(3, regroup_part(3, nc.vector.tensor_copy))
         for blk in range(BLOCKS):
             quantise_projection(blk, project_with_wk(blk))
 
@@ -192,7 +199,7 @@ def tile_crossattention_pa_s_kernel(tc, query, support, Wk, Wv, out):
             start=True,
             stop=True,
         )
-        hold_clock()
+        hold_clock(HOLD_PASSES)
 
         top = keep.tile([P, V], F32)
         nc.vector.tensor_reduce(
@@ -221,7 +228,7 @@ def tile_crossattention_pa_s_kernel(tc, query, support, Wk, Wv, out):
                     start=(c == 0),
                     stop=(c == D_PASSES - 1),
                 )
-        hold_clock()
+        hold_clock(HOLD_PASSES)
         val_t = keep.tile([P, SUP_BLOCKS, DV], F32)
         nc.scalar.copy(out=val_t[:], in_=val_ps[:])
 

@@ -17,6 +17,7 @@ AXIS = mybir.AxisListType
 P = 128
 PACK = 4
 K_PASS = P * PACK
+QUAD = 32
 
 B, N_SUP, D, DK, DV = 2, 16, 1024, 512, 128
 U = 64
@@ -24,12 +25,11 @@ V = 16
 D_PASSES = D // K_PASS
 KEY_CHUNKS = DK // P
 VAL_CHUNK = KEY_CHUNKS
-SUP_BLOCKS = N_SUP * V // P
-BLOCKS = 1 + SUP_BLOCKS
-IMAGES_PER_SUP_BLOCK = N_SUP // SUP_BLOCKS
-PARTS = [(blk, 0, D_PASSES) for blk in range(BLOCKS - 1)] + [(BLOCKS - 1, c, 1) for c in range(D_PASSES)]
-HOLD_PASSES = 2
-START_PASSES = 4
+HALVES = 2
+VH = V // HALVES
+SUP_COLS = N_SUP * V
+HOLD_PASSES = 8
+START_PASSES = 14
 
 FLOPS = 2 * D * (DK * (B * U + N_SUP * V) + DV * N_SUP * V) + 2 * DK * B * U * N_SUP * V
 
@@ -38,8 +38,8 @@ def pass_cols(c):
     return slice(c * P, (c + 1) * P)
 
 
-def block_cols(blk):
-    return slice(blk * P, (blk + 1) * P)
+def block_cols(h):
+    return slice(h * P, (h + 1) * P)
 
 
 def tile_crossattention_pa_s_kernel(tc, query, support, Wk, Wv, out):
@@ -48,59 +48,57 @@ def tile_crossattention_pa_s_kernel(tc, query, support, Wk, Wv, out):
         ctx.enter_context(tc.manual_schedule())
         const = ctx.enter_context(tc.tile_pool(name="const", bufs=1))
         keep = ctx.enter_context(tc.tile_pool(name="keep", bufs=1))
-        raws = ctx.enter_context(tc.tile_pool(name="raws", bufs=len(PARTS)))
         stage = ctx.enter_context(tc.tile_pool(name="stage", bufs=3))
         flip_psum = ctx.enter_context(tc.psum_pool(name="flip_psum", bufs=2))
-        proj_psum = ctx.enter_context(tc.psum_pool(name="proj_psum", bufs=BLOCKS))
+        proj_psum = ctx.enter_context(tc.psum_pool(name="proj_psum", bufs=HALVES + 1))
         tail_psum = ctx.enter_context(tc.psum_pool(name="tail_psum", bufs=1))
 
+        sup_raw = keep.tile([P, D_PASSES, QUAD * 2 * V], BF16)
+        sup_view = support.rearrange("n (c u g r) h w -> g u n c (r h w)", c=D_PASSES, u=2, g=P // QUAD)
+        for g in (0, 2, 1, 3):
+            for u in range(2):
+                nc.sync.dma_start(
+                    out=sup_raw[g * QUAD + u : (g + 1) * QUAD : 2, :, :],
+                    in_=sup_view[g, u],
+                )
         w_rows = keep.tile([P, KEY_CHUNKS + 1, D], BF16)
         wk_view = Wk.rearrange("(p t) d -> p t d", t=KEY_CHUNKS)
-        half = KEY_CHUNKS // 2
         for t in range(KEY_CHUNKS):
             nc.sync.dma_start(out=w_rows[:, t, :], in_=wk_view[:, t, :])
-
-        block_images = [query] + [
-            support[h * IMAGES_PER_SUP_BLOCK : (h + 1) * IMAGES_PER_SUP_BLOCK] for h in range(SUP_BLOCKS)
-        ]
-        raw_parts = []
-        for blk, first_pass, n_passes in PARTS:
-            images = block_images[blk]
-            channels = slice(first_pass * K_PASS, (first_pass + n_passes) * K_PASS)
-            raw = raws.tile([P, n_passes * K_PASS], BF16)
-            nc.sync.dma_start(
-                out=raw[:].rearrange("p (i c f) -> p i c f", i=images.shape[0], c=n_passes),
-                in_=images[:, channels].rearrange("i (c p j) h w -> p i c (j h w)", c=n_passes, j=PACK),
-            )
-            raw_parts.append(raw)
+        q_raw = keep.tile([P, D_PASSES * K_PASS], BF16)
+        nc.sync.dma_start(
+            out=q_raw[:].rearrange("p (i c u f) -> p i c u f", i=B, c=D_PASSES, u=2),
+            in_=query.rearrange("i (c u p e) h w -> p i c u (e h w)", c=D_PASSES, u=2, p=P),
+        )
         nc.sync.dma_start(out=w_rows[:, VAL_CHUNK, :], in_=Wv)
 
         ident = const.tile([P, P], F32)
         make_identity(nc, ident[:])
-        zeros = const.tile([P, K_PASS * PACK], BF16, align_bytes=64)
-        idle_codes = const.tile([P, K_PASS], U32, align_bytes=64)
-        idle_scales = const.tile([P, K_PASS], U8, align_bytes=64)
+        zeros = const.tile([P, K_PASS], BF16, align_bytes=64)
+        idle_codes = const.tile([P, P], U32, align_bytes=64)
+        idle_scales = const.tile([P, P], U8, align_bytes=64)
         nc.vector.memset(zeros[:].bitcast(I32), 0)
         nc.vector.quantize_mx(out=idle_codes[:].bitcast(FP8X4), scales=idle_scales[:], in_=zeros[:])
-        idle_ps = tail_psum.tile([P, K_PASS], F32)
+        idle_ps = tail_psum.tile([P, P], F32)
 
         def hold_clock(n_passes):
             for i in range(n_passes):
                 nc.tensor.matmul_mx(
                     out=idle_ps[:],
-                    lhsT=idle_codes[:, 0:P].bitcast(FP8X4),
-                    lhsT_scale=idle_scales[:, 0:P],
+                    lhsT=idle_codes[:].bitcast(FP8X4),
+                    lhsT_scale=idle_scales[:],
                     rhs=idle_codes[:].bitcast(FP8X4),
                     rhs_scale=idle_scales[:],
                     start=True,
                     stop=True,
                 )
 
-        same_pos = const.tile([P, V], F32)
+        hold_clock(START_PASSES)
+        same_pos = const.tile([P, VH], F32)
         nc.vector.tensor_reduce(
-            out=same_pos[:], in_=ident[:].rearrange("p (i v) -> p v i", v=V), axis=AXIS.X, op=ALU.add
+            out=same_pos[:], in_=ident[:].rearrange("p (v n) -> p v n", n=N_SUP), axis=AXIS.X, op=ALU.add
         )
-        inv_sum = const.tile([P, B, V], F32)
+        inv_sum = const.tile([P, HALVES, B, VH], F32)
         nc.vector.memset(inv_sum[:], 0.0)
         zero_col = const.tile([P, 1], F32)
         one_col = const.tile([P, 1], F32)
@@ -109,13 +107,15 @@ def tile_crossattention_pa_s_kernel(tc, query, support, Wk, Wv, out):
 
         w_codes = keep.tile([P, KEY_CHUNKS + 1, D_PASSES * P], U32, align_bytes=64)
         w_scales = keep.tile([P, KEY_CHUNKS + 1, D_PASSES * P], U8, align_bytes=64)
-        x_codes = keep.tile([P, BLOCKS, D_PASSES * P], U32, align_bytes=64)
-        x_scales = keep.tile([P, BLOCKS, D_PASSES * P], U8, align_bytes=64)
-        proj_codes = keep.tile([P, BLOCKS * P], U32, align_bytes=64)
-        proj_scales = keep.tile([P, BLOCKS * P], U8, align_bytes=64)
+        q_codes = keep.tile([P, D_PASSES * P], U32, align_bytes=64)
+        q_scales = keep.tile([P, D_PASSES * P], U8, align_bytes=64)
+        s_codes = keep.tile([P, D_PASSES, SUP_COLS], U32, align_bytes=64)
+        s_scales = keep.tile([P, D_PASSES, SUP_COLS], U8, align_bytes=64)
+        proj_codes = keep.tile([P, (1 + HALVES) * P], U32, align_bytes=64)
+        proj_scales = keep.tile([P, (1 + HALVES) * P], U8, align_bytes=64)
 
         def flip_weight_chunk(t):
-            words = w_rows[:, t, :].bitcast(F32).rearrange("p (c q u) -> p c u q", c=D_PASSES, u=2)
+            words = w_rows[:, t, :].bitcast(F32).rearrange("p (c u q) -> p c u q", c=D_PASSES, u=2)
             flipped = flip_psum.tile([P, D_PASSES, 2, P], F32)
             for c in range(D_PASSES):
                 for u in range(2):
@@ -130,141 +130,185 @@ def tile_crossattention_pa_s_kernel(tc, query, support, Wk, Wv, out):
         def quantise_weight_chunk(t, w_grouped):
             nc.vector.quantize_mx(out=w_codes[:, t, :].bitcast(FP8X4), scales=w_scales[:, t, :], in_=w_grouped[:])
 
-        def regroup_part(part, copy):
-            blk, first_pass, n_passes = PARTS[part]
-            n_images = block_images[blk].shape[0]
-            x_grouped = stage.tile([P, n_passes * K_PASS], BF16, align_bytes=64, tag="x_grouped")
-            grouped_view = x_grouped[:].rearrange("p (c i s j) -> p c i s j", c=n_passes, i=n_images, j=PACK)
-            raw_view = raw_parts[part][:].rearrange("p (i c j s) -> p c i s j", c=n_passes, i=n_images, j=PACK)
-            for c in range(n_passes):
-                copy(out=grouped_view[:, c], in_=raw_view[:, c])
-            return x_grouped
+        turned = keep.tile([P, D_PASSES, QUAD * 2 * V], BF16, align_bytes=64)
+        sup_grouped = keep.tile([P, D_PASSES, QUAD * 2 * V], BF16, align_bytes=64)
 
-        def quantise_part(part, x_grouped):
-            blk, first_pass, n_passes = PARTS[part]
-            cols = slice(first_pass * P, (first_pass + n_passes) * P)
-            nc.vector.quantize_mx(
-                out=x_codes[:, blk, cols].bitcast(FP8X4), scales=x_scales[:, blk, cols], in_=x_grouped[:]
+        def turn_support(c, copy):
+            copy(
+                out=turned[:, c, :].rearrange("p (w i r) -> p w r i", w=V // PACK, i=PACK),
+                in_=sup_raw[:, c, :].rearrange("p (r w i) -> p w r i", w=V // PACK, i=PACK),
             )
 
-        def project_with_wk(blk):
-            proj = proj_psum.tile([P, KEY_CHUNKS, P], F32)
-            for t in range(KEY_CHUNKS):
-                for c in range(D_PASSES):
-                    nc.tensor.matmul_mx(
-                        out=proj[:, t, :],
-                        lhsT=w_codes[:, t, pass_cols(c)].bitcast(FP8X4),
-                        lhsT_scale=w_scales[:, t, pass_cols(c)],
-                        rhs=x_codes[:, blk, pass_cols(c)].bitcast(FP8X4),
-                        rhs_scale=x_scales[:, blk, pass_cols(c)],
-                        start=(c == 0),
-                        stop=(c == D_PASSES - 1),
-                    )
+        def transpose_support(c):
+            nc.vector.transpose(sup_grouped[:, c, :].bitcast(F32), turned[:, c, :].bitcast(F32))
+
+        def quantise_support(c):
+            nc.vector.quantize_mx(
+                out=s_codes[:, c, :].bitcast(FP8X4), scales=s_scales[:, c, :], in_=sup_grouped[:, c, :]
+            )
+
+        q_grouped = keep.tile([P, D_PASSES * K_PASS], BF16, align_bytes=64)
+
+        def regroup_query(c, copy):
+            copy(
+                out=q_grouped[:].rearrange("p (c i s j) -> p c i s j", c=D_PASSES, i=B, j=PACK)[:, c],
+                in_=q_raw[:].rearrange("p (i c j s) -> p c i s j", c=D_PASSES, i=B, j=PACK)[:, c],
+            )
+
+        def project(proj, t, codes, scales):
+            for c in range(D_PASSES):
+                nc.tensor.matmul_mx(
+                    out=proj[:, t, :],
+                    lhsT=w_codes[:, t, pass_cols(c)].bitcast(FP8X4),
+                    lhsT_scale=w_scales[:, t, pass_cols(c)],
+                    rhs=codes[c].bitcast(FP8X4),
+                    rhs_scale=scales[c],
+                    start=(c == 0),
+                    stop=(c == D_PASSES - 1),
+                )
+
+        def round_projection(proj, copy):
             proj_grouped = stage.tile([P, P * PACK], BF16, align_bytes=64)
-            nc.scalar.copy(
+            copy(
                 out=proj_grouped[:].rearrange("p (w t) -> p w t", t=PACK), in_=proj[:].rearrange("p t w -> p w t")
             )
             return proj_grouped
 
         def quantise_projection(blk, proj_grouped):
+            cols = slice(blk * P, (blk + 1) * P)
             nc.vector.quantize_mx(
-                out=proj_codes[:, block_cols(blk)].bitcast(FP8X4),
-                scales=proj_scales[:, block_cols(blk)],
-                in_=proj_grouped[:],
+                out=proj_codes[:, cols].bitcast(FP8X4), scales=proj_scales[:, cols], in_=proj_grouped[:]
             )
 
-        for t in range(0, half):
-            quantise_weight_chunk(t, flip_weight_chunk(t))
-        quantise_part(0, regroup_part(0, nc.vector.tensor_copy))
-        for t in range(half, KEY_CHUNKS):
-            quantise_weight_chunk(t, flip_weight_chunk(t))
-        hold_clock(START_PASSES)
-        whole_block = regroup_part(1, nc.scalar.copy)
-        quantise_part(2, regroup_part(2, nc.vector.tensor_copy))
-        quantise_part(1, whole_block)
-        quantise_part(3, regroup_part(3, nc.vector.tensor_copy))
-        for blk in range(BLOCKS):
-            quantise_projection(blk, project_with_wk(blk))
+        turn_support(0, nc.vector.tensor_copy)
+        turn_support(1, nc.scalar.copy)
+        transpose_support(0)
+        transpose_support(1)
+        w_grouped = [flip_weight_chunk(t) for t in range(2)]
+        hold_clock(HOLD_PASSES)
+        quantise_support(0)
+        quantise_support(1)
+        quantise_weight_chunk(0, w_grouped[0])
+        quantise_weight_chunk(1, w_grouped[1])
+
+        sup_codes = [[s_codes[:, c, block_cols(h)] for c in range(D_PASSES)] for h in range(HALVES)]
+        sup_scales = [[s_scales[:, c, block_cols(h)] for c in range(D_PASSES)] for h in range(HALVES)]
+        key_ps = [proj_psum.tile([P, KEY_CHUNKS, P], F32, name="key_ps%d" % h, tag="proj") for h in range(HALVES)]
+        late_grouped = [flip_weight_chunk(t) for t in range(2, KEY_CHUNKS)]
+        for t in range(2):
+            for h in range(HALVES):
+                project(key_ps[h], t, sup_codes[h], sup_scales[h])
+        quantise_weight_chunk(2, late_grouped[0])
+        regroup_query(0, nc.vector.tensor_copy)
+        regroup_query(1, nc.scalar.copy)
+        quantise_weight_chunk(3, late_grouped[1])
+        nc.vector.quantize_mx(out=q_codes[:].bitcast(FP8X4), scales=q_scales[:], in_=q_grouped[:])
+        for t in range(2, KEY_CHUNKS):
+            for h in range(HALVES):
+                project(key_ps[h], t, sup_codes[h], sup_scales[h])
+        q_ps = proj_psum.tile([P, KEY_CHUNKS, P], F32, tag="proj")
+        for t in range(KEY_CHUNKS):
+            project(
+                q_ps,
+                t,
+                [q_codes[:, pass_cols(c)] for c in range(D_PASSES)],
+                [q_scales[:, pass_cols(c)] for c in range(D_PASSES)],
+            )
+        key0 = round_projection(key_ps[0], nc.scalar.copy)
+        key1 = round_projection(key_ps[1], nc.vector.tensor_copy)
+        quantise_projection(1, key0)
+        quantise_projection(2, key1)
+        quantise_projection(0, round_projection(q_ps, nc.scalar.copy))
 
         wv_grouped = flip_weight_chunk(VAL_CHUNK)
 
-        key_cols = slice(P, BLOCKS * P)
-        scores = tail_psum.tile([P, N_SUP * V], F32, tag="chain")
+        scores = tail_psum.tile([P, SUP_COLS], F32, tag="chain")
         nc.tensor.matmul_mx(
             out=scores[:],
-            lhsT=proj_codes[:, block_cols(0)].bitcast(FP8X4),
-            lhsT_scale=proj_scales[:, block_cols(0)],
-            rhs=proj_codes[:, key_cols].bitcast(FP8X4),
-            rhs_scale=proj_scales[:, key_cols],
+            lhsT=proj_codes[:, 0:P].bitcast(FP8X4),
+            lhsT_scale=proj_scales[:, 0:P],
+            rhs=proj_codes[:, P:].bitcast(FP8X4),
+            rhs_scale=proj_scales[:, P:],
             start=True,
             stop=True,
         )
         hold_clock(HOLD_PASSES)
+        quantise_weight_chunk(VAL_CHUNK, wv_grouped)
 
         top = keep.tile([P, V], F32)
-        nc.vector.tensor_reduce(
-            out=top[:], in_=scores[:].rearrange("p (n v) -> p v n", v=V), axis=AXIS.X, op=ALU.max
-        )
-        shifted = keep.tile([P, N_SUP * V], F32)
-        nc.vector.tensor_tensor(
-            out=shifted[:].rearrange("p (n v) -> p n v", v=V),
-            in0=scores[:].rearrange("p (n v) -> p n v", v=V),
-            in1=top[:].unsqueeze(1).to_broadcast([P, N_SUP, V]),
-            op=ALU.subtract,
-        )
-        expd = keep.tile([P, N_SUP * V], F32)
-        nc.scalar.activation(out=expd[:], in_=shifted[:], func=FUNC.Exp, scale=1.0 / math.sqrt(DK))
+        shifted = keep.tile([P, SUP_COLS], F32)
+        expd = keep.tile([P, SUP_COLS], F32)
+        sums = keep.tile([P, V], F32)
 
-        quantise_weight_chunk(VAL_CHUNK, wv_grouped)
-        val_ps = tail_psum.tile([P, SUP_BLOCKS, DV], F32)
-        for h in range(SUP_BLOCKS):
+        def by_position(x, h):
+            return x[:, block_cols(h)].rearrange("p (v n) -> p v n", n=N_SUP)
+
+        def positions(h):
+            return slice(h * VH, (h + 1) * VH)
+
+        for h in range(HALVES):
+            nc.vector.tensor_reduce(out=top[:, positions(h)], in_=by_position(scores, h), axis=AXIS.X, op=ALU.max)
+        for h in range(HALVES):
+            nc.vector.tensor_tensor(
+                out=by_position(shifted, h),
+                in0=by_position(scores, h),
+                in1=top[:, positions(h)].unsqueeze(2).to_broadcast([P, VH, N_SUP]),
+                op=ALU.subtract,
+            )
+        for h in range(HALVES):
+            nc.scalar.activation(
+                out=expd[:, block_cols(h)], in_=shifted[:, block_cols(h)], func=FUNC.Exp, scale=1.0 / math.sqrt(DK)
+            )
+
+        val_ps = tail_psum.tile([P, HALVES, DV], F32)
+        for h in range(HALVES):
             for c in range(D_PASSES):
                 nc.tensor.matmul_mx(
                     out=val_ps[:, h, :],
-                    lhsT=x_codes[:, 1 + h, pass_cols(c)].bitcast(FP8X4),
-                    lhsT_scale=x_scales[:, 1 + h, pass_cols(c)],
+                    lhsT=sup_codes[h][c].bitcast(FP8X4),
+                    lhsT_scale=sup_scales[h][c],
                     rhs=w_codes[:, VAL_CHUNK, pass_cols(c)].bitcast(FP8X4),
                     rhs_scale=w_scales[:, VAL_CHUNK, pass_cols(c)],
                     start=(c == 0),
                     stop=(c == D_PASSES - 1),
                 )
         hold_clock(HOLD_PASSES)
-        val_t = keep.tile([P, SUP_BLOCKS, DV], F32)
+        val_t = keep.tile([P, HALVES, DV], F32)
         nc.scalar.copy(out=val_t[:], in_=val_ps[:])
 
-        sums = keep.tile([P, V], F32)
-        nc.vector.tensor_reduce(
-            out=sums[:], in_=expd[:].rearrange("p (n v) -> p v n", v=V), axis=AXIS.X, op=ALU.add
-        )
-        for b in range(B):
-            own = slice(b * U, (b + 1) * U)
-            nc.vector.reciprocal(out=inv_sum[own, b, :], in_=sums[own, :])
+        for h in range(HALVES):
+            nc.vector.tensor_reduce(out=sums[:, positions(h)], in_=by_position(expd, h), axis=AXIS.X, op=ALU.add)
+        for h in range(HALVES):
+            for b in range(B):
+                own = slice(b * U, (b + 1) * U)
+                nc.vector.reciprocal(out=inv_sum[own, h, b, :], in_=sums[own, positions(h)])
 
+        result = keep.tile([P, B, V], F32)
         weights = []
-        for h in range(SUP_BLOCKS):
-            crossed = flip_psum.tile([P, B, V], F32, tag="flipped")
+        for h in range(HALVES):
+            crossed = flip_psum.tile([P, B, VH], F32, tag="flipped")
             nc.tensor.matmul(
                 out=crossed[:].rearrange("p b v -> p (b v)"),
-                lhsT=expd[:, h * P : (h + 1) * P],
-                rhs=inv_sum[:].rearrange("p b v -> p (b v)"),
+                lhsT=expd[:, block_cols(h)],
+                rhs=inv_sum[:, h].rearrange("p b v -> p (b v)"),
                 start=True,
                 stop=True,
             )
-            weight = keep.tile([P, B, V], F32, name="weight%d" % h)
+            weight = keep.tile([P, B, VH], F32, name="weight%d" % h)
             nc.vector.tensor_tensor(
-                out=weight[:], in0=crossed[:], in1=same_pos[:].unsqueeze(1).to_broadcast([P, B, V]), op=ALU.mult
+                out=weight[:], in0=crossed[:], in1=same_pos[:].unsqueeze(1).to_broadcast([P, B, VH]), op=ALU.mult
             )
             weights.append(weight)
-
-        result_ps = tail_psum.tile([P, B * V], F32, tag="chain")
-        for h in range(SUP_BLOCKS):
+        result_ps = tail_psum.tile([P, HALVES, B, VH], F32, tag="chain")
+        for h in range(HALVES):
             nc.tensor.matmul(
-                out=result_ps[:],
+                out=result_ps[:, h].rearrange("p b v -> p (b v)"),
                 lhsT=val_t[:, h, :],
                 rhs=weights[h][:].rearrange("p b v -> p (b v)"),
-                start=(h == 0),
-                stop=(h == SUP_BLOCKS - 1),
+                start=True,
+                stop=True,
             )
-        result = keep.tile([P, B, V], F32)
-        nc.vector.tensor_copy(out=result[:].rearrange("p b v -> p (b v)"), in_=result_ps[:])
+        nc.vector.tensor_copy(
+            out=result[:].rearrange("p b (h v) -> p b h v", h=HALVES), in_=result_ps[:].rearrange("p h b v -> p b h v")
+        )
         nc.sync.dma_start(out=out.rearrange("b c v -> c b v"), in_=result[:])

@@ -28,8 +28,9 @@ VAL_CHUNK = KEY_CHUNKS
 HALVES = 2
 VH = V // HALVES
 SUP_COLS = N_SUP * V
-HOLD_PASSES = 8
-START_PASSES = 14
+CHUNK_PASSES = (8, 0, 0, 8)
+HOLD_PASSES = 10
+START_PASSES = 18
 
 FLOPS = 2 * D * (DK * (B * U + N_SUP * V) + DV * N_SUP * V) + 2 * DK * B * U * N_SUP * V
 
@@ -49,22 +50,28 @@ def tile_crossattention_pa_s_kernel(tc, query, support, Wk, Wv, out):
         const = ctx.enter_context(tc.tile_pool(name="const", bufs=1))
         keep = ctx.enter_context(tc.tile_pool(name="keep", bufs=1))
         stage = ctx.enter_context(tc.tile_pool(name="stage", bufs=3))
-        flip_psum = ctx.enter_context(tc.psum_pool(name="flip_psum", bufs=2))
+        flip_psum = ctx.enter_context(tc.psum_pool(name="flip_psum", bufs=3))
         proj_psum = ctx.enter_context(tc.psum_pool(name="proj_psum", bufs=HALVES + 1))
         tail_psum = ctx.enter_context(tc.psum_pool(name="tail_psum", bufs=1))
 
         sup_raw = keep.tile([P, D_PASSES, QUAD * 2 * V], BF16)
         sup_view = support.rearrange("n (c u g r) h w -> g u n c (r h w)", c=D_PASSES, u=2, g=P // QUAD)
-        for g in (0, 2, 1, 3):
-            for u in range(2):
-                nc.sync.dma_start(
-                    out=sup_raw[g * QUAD + u : (g + 1) * QUAD : 2, :, :],
-                    in_=sup_view[g, u],
-                )
+
+        def load_support(queue, g, u):
+            queue.dma_start(out=sup_raw[g * QUAD + u : (g + 1) * QUAD : 2, :, :], in_=sup_view[g, u])
+
         w_rows = keep.tile([P, KEY_CHUNKS + 1, D], BF16)
         wk_view = Wk.rearrange("(p t) d -> p t d", t=KEY_CHUNKS)
-        for t in range(KEY_CHUNKS):
+
+        def load_key_chunk(t):
             nc.sync.dma_start(out=w_rows[:, t, :], in_=wk_view[:, t, :])
+
+        support_loads = [(g, u) for g in (0, 2, 1, 3) for u in range(2)]
+        load_support(nc.gpsimd, *support_loads[-1])
+        for g, u in support_loads[:-1]:
+            load_support(nc.sync, g, u)
+        for t in range(KEY_CHUNKS):
+            load_key_chunk(t)
         q_raw = keep.tile([P, D_PASSES * K_PASS], BF16)
         nc.sync.dma_start(
             out=q_raw[:].rearrange("p (i c u f) -> p i c u f", i=B, c=D_PASSES, u=2),
@@ -79,12 +86,12 @@ def tile_crossattention_pa_s_kernel(tc, query, support, Wk, Wv, out):
         idle_scales = const.tile([P, P], U8, align_bytes=64)
         nc.vector.memset(zeros[:].bitcast(I32), 0)
         nc.vector.quantize_mx(out=idle_codes[:].bitcast(FP8X4), scales=idle_scales[:], in_=zeros[:])
-        idle_ps = tail_psum.tile([P, P], F32)
+        idle_ps = proj_psum.tile([P, KEY_CHUNKS, P], F32, tag="proj")
 
-        def hold_clock(n_passes):
+        def hold_clock(n_passes, idle_ps=idle_ps):
             for i in range(n_passes):
                 nc.tensor.matmul_mx(
-                    out=idle_ps[:],
+                    out=idle_ps[:, 0, :],
                     lhsT=idle_codes[:].bitcast(FP8X4),
                     lhsT_scale=idle_scales[:],
                     rhs=idle_codes[:].bitcast(FP8X4),
@@ -133,10 +140,10 @@ def tile_crossattention_pa_s_kernel(tc, query, support, Wk, Wv, out):
         turned = keep.tile([P, D_PASSES, QUAD * 2 * V], BF16, align_bytes=64)
         sup_grouped = keep.tile([P, D_PASSES, QUAD * 2 * V], BF16, align_bytes=64)
 
-        def turn_support(c, copy):
+        def turn_support(c, copy, groups):
             copy(
-                out=turned[:, c, :].rearrange("p (w i r) -> p w r i", w=V // PACK, i=PACK),
-                in_=sup_raw[:, c, :].rearrange("p (r w i) -> p w r i", w=V // PACK, i=PACK),
+                out=turned[:, c, :].rearrange("p (w i r) -> p w r i", w=V // PACK, i=PACK)[:, groups],
+                in_=sup_raw[:, c, :].rearrange("p (r w i) -> p w r i", w=V // PACK, i=PACK)[:, groups],
             )
 
         def transpose_support(c):
@@ -180,12 +187,14 @@ def tile_crossattention_pa_s_kernel(tc, query, support, Wk, Wv, out):
                 out=proj_codes[:, cols].bitcast(FP8X4), scales=proj_scales[:, cols], in_=proj_grouped[:]
             )
 
-        turn_support(0, nc.vector.tensor_copy)
-        turn_support(1, nc.scalar.copy)
+        turn_support(0, nc.vector.tensor_copy, slice(0, 4))
+        turn_support(1, nc.vector.tensor_copy, slice(0, 4))
         transpose_support(0)
         transpose_support(1)
-        w_grouped = [flip_weight_chunk(t) for t in range(2)]
-        hold_clock(HOLD_PASSES)
+        w_grouped = []
+        for t in range(2):
+            w_grouped.append(flip_weight_chunk(t))
+            hold_clock(CHUNK_PASSES[t])
         quantise_support(0)
         quantise_support(1)
         quantise_weight_chunk(0, w_grouped[0])
@@ -194,7 +203,10 @@ def tile_crossattention_pa_s_kernel(tc, query, support, Wk, Wv, out):
         sup_codes = [[s_codes[:, c, block_cols(h)] for c in range(D_PASSES)] for h in range(HALVES)]
         sup_scales = [[s_scales[:, c, block_cols(h)] for c in range(D_PASSES)] for h in range(HALVES)]
         key_ps = [proj_psum.tile([P, KEY_CHUNKS, P], F32, name="key_ps%d" % h, tag="proj") for h in range(HALVES)]
-        late_grouped = [flip_weight_chunk(t) for t in range(2, KEY_CHUNKS)]
+        late_grouped = []
+        for t in range(2, KEY_CHUNKS):
+            late_grouped.append(flip_weight_chunk(t))
+            hold_clock(CHUNK_PASSES[t])
         for t in range(2):
             for h in range(HALVES):
                 project(key_ps[h], t, sup_codes[h], sup_scales[h])
@@ -222,6 +234,9 @@ def tile_crossattention_pa_s_kernel(tc, query, support, Wk, Wv, out):
 
         wv_grouped = flip_weight_chunk(VAL_CHUNK)
 
+        idle_tail = proj_psum.tile([P, KEY_CHUNKS, P], F32, tag="proj")
+        hold_clock(6, idle_tail)
+
         scores = tail_psum.tile([P, SUP_COLS], F32, tag="chain")
         nc.tensor.matmul_mx(
             out=scores[:],
@@ -232,7 +247,7 @@ def tile_crossattention_pa_s_kernel(tc, query, support, Wk, Wv, out):
             start=True,
             stop=True,
         )
-        hold_clock(HOLD_PASSES)
+        hold_clock(HOLD_PASSES, idle_tail)
         quantise_weight_chunk(VAL_CHUNK, wv_grouped)
 
         top = keep.tile([P, V], F32)
@@ -272,7 +287,7 @@ def tile_crossattention_pa_s_kernel(tc, query, support, Wk, Wv, out):
                     start=(c == 0),
                     stop=(c == D_PASSES - 1),
                 )
-        hold_clock(HOLD_PASSES)
+        hold_clock(HOLD_PASSES, idle_tail)
         val_t = keep.tile([P, HALVES, DV], F32)
         nc.scalar.copy(out=val_t[:], in_=val_ps[:])
 

@@ -66,11 +66,14 @@ def tile_crossattention_pa_s_kernel(tc, query, support, Wk, Wv, out):
         def load_key_chunk(t):
             nc.sync.dma_start(out=w_rows[:, t, :], in_=wk_view[:, t, :])
 
-        support_loads = [(g, u) for g in (0, 2, 1, 3) for u in range(2)]
-        load_support(nc.gpsimd, *support_loads[-1])
-        for g, u in support_loads[:-1]:
+        for g in (2, 3):
+            for u in range(2):
+                load_support(nc.scalar, g, u)
+        for g, u in ((0, 0), (0, 1), (1, 0)):
             load_support(nc.sync, g, u)
-        for t in range(KEY_CHUNKS):
+        load_key_chunk(0)
+        load_support(nc.sync, 1, 1)
+        for t in range(1, KEY_CHUNKS):
             load_key_chunk(t)
         q_raw = keep.tile([P, D_PASSES * K_PASS], BF16)
         nc.sync.dma_start(
@@ -188,7 +191,7 @@ def tile_crossattention_pa_s_kernel(tc, query, support, Wk, Wv, out):
             )
 
         turn_support(0, nc.vector.tensor_copy, slice(0, 4))
-        turn_support(1, nc.vector.tensor_copy, slice(0, 4))
+        turn_support(1, nc.scalar.copy, slice(0, 4))
         transpose_support(0)
         transpose_support(1)
         w_grouped = []

@@ -28,9 +28,8 @@ VAL_CHUNK = KEY_CHUNKS
 HALVES = 2
 VH = V // HALVES
 SUP_COLS = N_SUP * V
-CHUNK_PASSES = (8, 0, 0, 8)
-HOLD_PASSES = 10
-START_PASSES = 18
+CHUNK_PASSES = (2, 5, 2, 4)
+START_PASSES = 16
 
 FLOPS = 2 * D * (DK * (B * U + N_SUP * V) + DV * N_SUP * V) + 2 * DK * B * U * N_SUP * V
 
@@ -49,16 +48,16 @@ def tile_crossattention_pa_s_kernel(tc, query, support, Wk, Wv, out):
         ctx.enter_context(tc.manual_schedule())
         const = ctx.enter_context(tc.tile_pool(name="const", bufs=1))
         keep = ctx.enter_context(tc.tile_pool(name="keep", bufs=1))
-        stage = ctx.enter_context(tc.tile_pool(name="stage", bufs=3))
-        flip_psum = ctx.enter_context(tc.psum_pool(name="flip_psum", bufs=3))
-        proj_psum = ctx.enter_context(tc.psum_pool(name="proj_psum", bufs=HALVES + 1))
+        stage = ctx.enter_context(tc.tile_pool(name="stage", bufs=KEY_CHUNKS))
+        flip_psum = ctx.enter_context(tc.psum_pool(name="flip_psum", bufs=2))
+        proj_psum = ctx.enter_context(tc.psum_pool(name="proj_psum", bufs=5))
         tail_psum = ctx.enter_context(tc.psum_pool(name="tail_psum", bufs=1))
 
         sup_raw = keep.tile([P, D_PASSES, QUAD * 2 * V], BF16)
-        sup_view = support.rearrange("n (c u g r) h w -> g u n c (r h w)", c=D_PASSES, u=2, g=P // QUAD)
+        sup_view = support.rearrange("n (c u g r) h w -> g c n u (r h w)", c=D_PASSES, u=2, g=P // QUAD)
 
-        def load_support(queue, g, u):
-            queue.dma_start(out=sup_raw[g * QUAD + u : (g + 1) * QUAD : 2, :, :], in_=sup_view[g, u])
+        def load_support(queue, g, c):
+            queue.dma_start(out=sup_raw[g * QUAD : (g + 1) * QUAD, c, :], in_=sup_view[g, c])
 
         w_rows = keep.tile([P, KEY_CHUNKS + 1, D], BF16)
         wk_view = Wk.rearrange("(p t) d -> p t d", t=KEY_CHUNKS)
@@ -66,20 +65,23 @@ def tile_crossattention_pa_s_kernel(tc, query, support, Wk, Wv, out):
         def load_key_chunk(t):
             nc.sync.dma_start(out=w_rows[:, t, :], in_=wk_view[:, t, :])
 
-        for g in (2, 3):
-            for u in range(2):
-                load_support(nc.scalar, g, u)
-        for g, u in ((0, 0), (0, 1), (1, 0)):
-            load_support(nc.sync, g, u)
+        for g, c in ((2, 0), (3, 0), (2, 1)):
+            load_support(nc.scalar, g, c)
+        for g in range(2):
+            load_support(nc.sync, g, 0)
         load_key_chunk(0)
-        load_support(nc.sync, 1, 1)
-        for t in range(1, KEY_CHUNKS):
+        load_support(nc.sync, 0, 1)
+        load_key_chunk(1)
+        for g in (1, 3):
+            load_support(nc.sync, g, 1)
+        for t in range(2, KEY_CHUNKS):
             load_key_chunk(t)
         q_raw = keep.tile([P, D_PASSES * K_PASS], BF16)
-        nc.sync.dma_start(
-            out=q_raw[:].rearrange("p (i c u f) -> p i c u f", i=B, c=D_PASSES, u=2),
-            in_=query.rearrange("i (c u p e) h w -> p i c u (e h w)", c=D_PASSES, u=2, p=P),
-        )
+        for i in range(B):
+            nc.sync.dma_start(
+                out=q_raw[:].rearrange("p (i c u f) -> p i c u f", i=B, c=D_PASSES, u=2)[:, i],
+                in_=query.rearrange("i (c u p e) h w -> p i c u (e h w)", c=D_PASSES, u=2, p=P)[:, i],
+            )
         nc.sync.dma_start(out=w_rows[:, VAL_CHUNK, :], in_=Wv)
 
         ident = const.tile([P, P], F32)
@@ -143,10 +145,10 @@ def tile_crossattention_pa_s_kernel(tc, query, support, Wk, Wv, out):
         turned = keep.tile([P, D_PASSES, QUAD * 2 * V], BF16, align_bytes=64)
         sup_grouped = keep.tile([P, D_PASSES, QUAD * 2 * V], BF16, align_bytes=64)
 
-        def turn_support(c, copy, groups):
+        def turn_support(c, copy):
             copy(
-                out=turned[:, c, :].rearrange("p (w i r) -> p w r i", w=V // PACK, i=PACK)[:, groups],
-                in_=sup_raw[:, c, :].rearrange("p (r w i) -> p w r i", w=V // PACK, i=PACK)[:, groups],
+                out=turned[:, c, :].rearrange("p (w i r) -> p w r i", w=V // PACK, i=PACK),
+                in_=sup_raw[:, c, :].rearrange("p (r w i) -> p w r i", w=V // PACK, i=PACK),
             )
 
         def transpose_support(c):
@@ -159,16 +161,16 @@ def tile_crossattention_pa_s_kernel(tc, query, support, Wk, Wv, out):
 
         q_grouped = keep.tile([P, D_PASSES * K_PASS], BF16, align_bytes=64)
 
-        def regroup_query(c, copy):
+        def regroup_query(i, copy):
             copy(
-                out=q_grouped[:].rearrange("p (c i s j) -> p c i s j", c=D_PASSES, i=B, j=PACK)[:, c],
-                in_=q_raw[:].rearrange("p (i c j s) -> p c i s j", c=D_PASSES, i=B, j=PACK)[:, c],
+                out=q_grouped[:].rearrange("p (c i s j) -> p i c s j", c=D_PASSES, i=B, j=PACK)[:, i],
+                in_=q_raw[:].rearrange("p (i c j s) -> p i c s j", c=D_PASSES, i=B, j=PACK)[:, i],
             )
 
         def project(proj, t, codes, scales):
             for c in range(D_PASSES):
                 nc.tensor.matmul_mx(
-                    out=proj[:, t, :],
+                    out=proj,
                     lhsT=w_codes[:, t, pass_cols(c)].bitcast(FP8X4),
                     lhsT_scale=w_scales[:, t, pass_cols(c)],
                     rhs=codes[c].bitcast(FP8X4),
@@ -177,99 +179,108 @@ def tile_crossattention_pa_s_kernel(tc, query, support, Wk, Wv, out):
                     stop=(c == D_PASSES - 1),
                 )
 
-        def round_projection(proj, copy):
-            proj_grouped = stage.tile([P, P * PACK], BF16, align_bytes=64)
+        def round_projection(proj, copy, proj_grouped, cols, ts):
             copy(
-                out=proj_grouped[:].rearrange("p (w t) -> p w t", t=PACK), in_=proj[:].rearrange("p t w -> p w t")
+                out=proj_grouped[:].rearrange("p (w t) -> p w t", t=PACK)[:, cols, ts],
+                in_=proj[:].rearrange("p t w -> p w t"),
             )
-            return proj_grouped
 
-        def quantise_projection(blk, proj_grouped):
-            cols = slice(blk * P, (blk + 1) * P)
+        def quantise_projection(cols, proj_grouped):
             nc.vector.quantize_mx(
                 out=proj_codes[:, cols].bitcast(FP8X4), scales=proj_scales[:, cols], in_=proj_grouped[:]
             )
 
-        turn_support(0, nc.vector.tensor_copy, slice(0, 4))
-        turn_support(1, nc.scalar.copy, slice(0, 4))
+        turn_support(0, nc.vector.tensor_copy)
         transpose_support(0)
-        transpose_support(1)
+        quantise_support(0)
         w_grouped = []
-        for t in range(2):
+        for t in range(KEY_CHUNKS):
             w_grouped.append(flip_weight_chunk(t))
             hold_clock(CHUNK_PASSES[t])
-        quantise_support(0)
-        quantise_support(1)
+        turn_support(1, nc.vector.tensor_copy)
         quantise_weight_chunk(0, w_grouped[0])
+        transpose_support(1)
         quantise_weight_chunk(1, w_grouped[1])
+        quantise_support(1)
+        quantise_weight_chunk(2, w_grouped[2])
+        regroup_query(0, nc.scalar.copy)
+        quantise_weight_chunk(3, w_grouped[3])
+        regroup_query(1, nc.vector.tensor_copy)
+        nc.vector.quantize_mx(out=q_codes[:].bitcast(FP8X4), scales=q_scales[:], in_=q_grouped[:])
 
         sup_codes = [[s_codes[:, c, block_cols(h)] for c in range(D_PASSES)] for h in range(HALVES)]
         sup_scales = [[s_scales[:, c, block_cols(h)] for c in range(D_PASSES)] for h in range(HALVES)]
-        key_ps = [proj_psum.tile([P, KEY_CHUNKS, P], F32, name="key_ps%d" % h, tag="proj") for h in range(HALVES)]
-        late_grouped = []
-        for t in range(2, KEY_CHUNKS):
-            late_grouped.append(flip_weight_chunk(t))
-            hold_clock(CHUNK_PASSES[t])
+        early = slice(0, 2)
+        late = slice(2, KEY_CHUNKS)
+        key_early = proj_psum.tile([P, 2, SUP_COLS], F32, tag="proj")
         for t in range(2):
-            for h in range(HALVES):
-                project(key_ps[h], t, sup_codes[h], sup_scales[h])
-        quantise_weight_chunk(2, late_grouped[0])
-        regroup_query(0, nc.vector.tensor_copy)
-        regroup_query(1, nc.scalar.copy)
-        quantise_weight_chunk(3, late_grouped[1])
-        nc.vector.quantize_mx(out=q_codes[:].bitcast(FP8X4), scales=q_scales[:], in_=q_grouped[:])
+            project(
+                key_early[:, t, :],
+                t,
+                [s_codes[:, c, :] for c in range(D_PASSES)],
+                [s_scales[:, c, :] for c in range(D_PASSES)],
+            )
+        key_late = [proj_psum.tile([P, 2, P], F32, name="key_late%d" % h, tag="proj") for h in range(HALVES)]
         for t in range(2, KEY_CHUNKS):
             for h in range(HALVES):
-                project(key_ps[h], t, sup_codes[h], sup_scales[h])
-        q_ps = proj_psum.tile([P, KEY_CHUNKS, P], F32, tag="proj")
+                project(key_late[h][:, t - 2, :], t, sup_codes[h], sup_scales[h])
+        key_grouped = keep.tile([P, SUP_COLS * PACK], BF16, align_bytes=64)
+        round_projection(key_early, nc.scalar.copy, key_grouped, slice(0, SUP_COLS), early)
+        round_projection(key_late[0], nc.scalar.copy, key_grouped, block_cols(0), late)
+        round_projection(key_late[1], nc.vector.tensor_copy, key_grouped, block_cols(1), late)
+        wv_grouped = flip_weight_chunk(VAL_CHUNK)
+        q_ps = [proj_psum.tile([P, 2, P], F32, name="q_ps%d" % i, tag="proj") for i in range(2)]
         for t in range(KEY_CHUNKS):
             project(
-                q_ps,
+                q_ps[t // 2][:, t % 2, :],
                 t,
                 [q_codes[:, pass_cols(c)] for c in range(D_PASSES)],
                 [q_scales[:, pass_cols(c)] for c in range(D_PASSES)],
             )
-        key0 = round_projection(key_ps[0], nc.scalar.copy)
-        key1 = round_projection(key_ps[1], nc.vector.tensor_copy)
-        quantise_projection(1, key0)
-        quantise_projection(2, key1)
-        quantise_projection(0, round_projection(q_ps, nc.scalar.copy))
-
-        wv_grouped = flip_weight_chunk(VAL_CHUNK)
+        qp_grouped = keep.tile([P, P * PACK], BF16, align_bytes=64)
+        round_projection(q_ps[0], nc.vector.tensor_copy, qp_grouped, slice(0, P), early)
+        round_projection(q_ps[1], nc.scalar.copy, qp_grouped, slice(0, P), late)
+        quantise_projection(slice(P, (1 + HALVES) * P), key_grouped)
+        quantise_projection(slice(0, P), qp_grouped)
+        quantise_weight_chunk(VAL_CHUNK, wv_grouped)
 
         idle_tail = proj_psum.tile([P, KEY_CHUNKS, P], F32, tag="proj")
-        hold_clock(6, idle_tail)
+        hold_clock(4, idle_tail)
 
-        scores = tail_psum.tile([P, SUP_COLS], F32, tag="chain")
-        nc.tensor.matmul_mx(
-            out=scores[:],
-            lhsT=proj_codes[:, 0:P].bitcast(FP8X4),
-            lhsT_scale=proj_scales[:, 0:P],
-            rhs=proj_codes[:, P:].bitcast(FP8X4),
-            rhs_scale=proj_scales[:, P:],
-            start=True,
-            stop=True,
-        )
-        hold_clock(HOLD_PASSES, idle_tail)
-        quantise_weight_chunk(VAL_CHUNK, wv_grouped)
+        scores = [
+            tail_psum.tile([P, P], F32, name="scores0", tag="chain"),
+            proj_psum.tile([P, P], F32, name="scores1", tag="proj"),
+        ]
+        for h in range(HALVES):
+            key_cols = slice((1 + h) * P, (2 + h) * P)
+            nc.tensor.matmul_mx(
+                out=scores[h][:],
+                lhsT=proj_codes[:, 0:P].bitcast(FP8X4),
+                lhsT_scale=proj_scales[:, 0:P],
+                rhs=proj_codes[:, key_cols].bitcast(FP8X4),
+                rhs_scale=proj_scales[:, key_cols],
+                start=True,
+                stop=True,
+            )
+        hold_clock(4, idle_tail)
 
         top = keep.tile([P, V], F32)
         shifted = keep.tile([P, SUP_COLS], F32)
         expd = keep.tile([P, SUP_COLS], F32)
         sums = keep.tile([P, V], F32)
 
-        def by_position(x, h):
-            return x[:, block_cols(h)].rearrange("p (v n) -> p v n", n=N_SUP)
+        def by_position(x):
+            return x.rearrange("p (v n) -> p v n", n=N_SUP)
 
         def positions(h):
             return slice(h * VH, (h + 1) * VH)
 
         for h in range(HALVES):
-            nc.vector.tensor_reduce(out=top[:, positions(h)], in_=by_position(scores, h), axis=AXIS.X, op=ALU.max)
+            nc.vector.tensor_reduce(out=top[:, positions(h)], in_=by_position(scores[h][:]), axis=AXIS.X, op=ALU.max)
         for h in range(HALVES):
             nc.vector.tensor_tensor(
-                out=by_position(shifted, h),
-                in0=by_position(scores, h),
+                out=by_position(shifted[:, block_cols(h)]),
+                in0=by_position(scores[h][:]),
                 in1=top[:, positions(h)].unsqueeze(2).to_broadcast([P, VH, N_SUP]),
                 op=ALU.subtract,
             )
@@ -278,7 +289,7 @@ def tile_crossattention_pa_s_kernel(tc, query, support, Wk, Wv, out):
                 out=expd[:, block_cols(h)], in_=shifted[:, block_cols(h)], func=FUNC.Exp, scale=1.0 / math.sqrt(DK)
             )
 
-        val_ps = tail_psum.tile([P, HALVES, DV], F32)
+        val_ps = flip_psum.tile([P, HALVES, DV], F32, tag="flipped")
         for h in range(HALVES):
             for c in range(D_PASSES):
                 nc.tensor.matmul_mx(
@@ -290,12 +301,12 @@ def tile_crossattention_pa_s_kernel(tc, query, support, Wk, Wv, out):
                     start=(c == 0),
                     stop=(c == D_PASSES - 1),
                 )
-        hold_clock(HOLD_PASSES, idle_tail)
+        hold_clock(16, idle_tail)
         val_t = keep.tile([P, HALVES, DV], F32)
         nc.scalar.copy(out=val_t[:], in_=val_ps[:])
 
         for h in range(HALVES):
-            nc.vector.tensor_reduce(out=sums[:, positions(h)], in_=by_position(expd, h), axis=AXIS.X, op=ALU.add)
+            nc.vector.tensor_reduce(out=sums[:, positions(h)], in_=by_position(expd[:, block_cols(h)]), axis=AXIS.X, op=ALU.add)
         for h in range(HALVES):
             for b in range(B):
                 own = slice(b * U, (b + 1) * U)

@@ -28,8 +28,9 @@ VAL_CHUNK = KEY_CHUNKS
 HALVES = 2
 VH = V // HALVES
 SUP_COLS = N_SUP * V
-CHUNK_PASSES = (2, 5, 2, 4)
-START_PASSES = 16
+CHUNK_PASSES = (4, 4, 3)
+LAST_CHUNK_PASSES = 6
+START_PASSES = 18
 
 FLOPS = 2 * D * (DK * (B * U + N_SUP * V) + DV * N_SUP * V) + 2 * DK * B * U * N_SUP * V
 
@@ -105,6 +106,12 @@ def tile_crossattention_pa_s_kernel(tc, query, support, Wk, Wv, out):
                     stop=True,
                 )
 
+        def hold_clock_plain(n_matmuls):
+            for i in range(n_matmuls):
+                nc.tensor.matmul(
+                    out=idle_ps[:, 0, :], lhsT=zeros[:, 0:P], rhs=zeros[:, 0:P], start=True, stop=True
+                )
+
         hold_clock(START_PASSES)
         same_pos = const.tile([P, VH], F32)
         nc.vector.tensor_reduce(
@@ -161,10 +168,17 @@ def tile_crossattention_pa_s_kernel(tc, query, support, Wk, Wv, out):
 
         q_grouped = keep.tile([P, D_PASSES * K_PASS], BF16, align_bytes=64)
 
-        def regroup_query(i, copy):
+        def regroup_query(i, passes, copy):
             copy(
-                out=q_grouped[:].rearrange("p (c i s j) -> p i c s j", c=D_PASSES, i=B, j=PACK)[:, i],
-                in_=q_raw[:].rearrange("p (i c j s) -> p i c s j", c=D_PASSES, i=B, j=PACK)[:, i],
+                out=q_grouped[:].rearrange("p (c i s j) -> p i c s j", c=D_PASSES, i=B, j=PACK)[:, i, passes],
+                in_=q_raw[:].rearrange("p (i c j s) -> p i c s j", c=D_PASSES, i=B, j=PACK)[:, i, passes],
+            )
+
+        def quantise_query(c):
+            nc.vector.quantize_mx(
+                out=q_codes[:, pass_cols(c)].bitcast(FP8X4),
+                scales=q_scales[:, pass_cols(c)],
+                in_=q_grouped[:, c * K_PASS : (c + 1) * K_PASS],
             )
 
         def project(proj, t, codes, scales):
@@ -196,17 +210,21 @@ def tile_crossattention_pa_s_kernel(tc, query, support, Wk, Wv, out):
         w_grouped = []
         for t in range(KEY_CHUNKS):
             w_grouped.append(flip_weight_chunk(t))
-            hold_clock(CHUNK_PASSES[t])
+            if t < KEY_CHUNKS - 1:
+                hold_clock_plain(CHUNK_PASSES[t])
+        hold_clock(LAST_CHUNK_PASSES)
         turn_support(1, nc.vector.tensor_copy)
         quantise_weight_chunk(0, w_grouped[0])
         transpose_support(1)
         quantise_weight_chunk(1, w_grouped[1])
         quantise_support(1)
         quantise_weight_chunk(2, w_grouped[2])
-        regroup_query(0, nc.scalar.copy)
+        regroup_query(0, slice(0, D_PASSES), nc.vector.tensor_copy)
         quantise_weight_chunk(3, w_grouped[3])
-        regroup_query(1, nc.vector.tensor_copy)
-        nc.vector.quantize_mx(out=q_codes[:].bitcast(FP8X4), scales=q_scales[:], in_=q_grouped[:])
+        regroup_query(1, slice(0, 1), nc.vector.tensor_copy)
+        regroup_query(1, slice(1, 2), nc.scalar.copy)
+        for c in range(D_PASSES):
+            quantise_query(c)
 
         sup_codes = [[s_codes[:, c, block_cols(h)] for c in range(D_PASSES)] for h in range(HALVES)]
         sup_scales = [[s_scales[:, c, block_cols(h)] for c in range(D_PASSES)] for h in range(HALVES)]
@@ -228,7 +246,6 @@ def tile_crossattention_pa_s_kernel(tc, query, support, Wk, Wv, out):
         round_projection(key_early, nc.scalar.copy, key_grouped, slice(0, SUP_COLS), early)
         round_projection(key_late[0], nc.scalar.copy, key_grouped, block_cols(0), late)
         round_projection(key_late[1], nc.vector.tensor_copy, key_grouped, block_cols(1), late)
-        wv_grouped = flip_weight_chunk(VAL_CHUNK)
         q_ps = [proj_psum.tile([P, 2, P], F32, name="q_ps%d" % i, tag="proj") for i in range(2)]
         for t in range(KEY_CHUNKS):
             project(
@@ -242,7 +259,7 @@ def tile_crossattention_pa_s_kernel(tc, query, support, Wk, Wv, out):
         round_projection(q_ps[1], nc.scalar.copy, qp_grouped, slice(0, P), late)
         quantise_projection(slice(P, (1 + HALVES) * P), key_grouped)
         quantise_projection(slice(0, P), qp_grouped)
-        quantise_weight_chunk(VAL_CHUNK, wv_grouped)
+        wv_grouped = flip_weight_chunk(VAL_CHUNK)
 
         idle_tail = proj_psum.tile([P, KEY_CHUNKS, P], F32, tag="proj")
         hold_clock(4, idle_tail)
@@ -262,7 +279,7 @@ def tile_crossattention_pa_s_kernel(tc, query, support, Wk, Wv, out):
                 start=True,
                 stop=True,
             )
-        hold_clock(4, idle_tail)
+        hold_clock(10, idle_tail)
 
         top = keep.tile([P, V], F32)
         shifted = keep.tile([P, SUP_COLS], F32)
@@ -284,6 +301,7 @@ def tile_crossattention_pa_s_kernel(tc, query, support, Wk, Wv, out):
                 in1=top[:, positions(h)].unsqueeze(2).to_broadcast([P, VH, N_SUP]),
                 op=ALU.subtract,
             )
+        quantise_weight_chunk(VAL_CHUNK, wv_grouped)
         for h in range(HALVES):
             nc.scalar.activation(
                 out=expd[:, block_cols(h)], in_=shifted[:, block_cols(h)], func=FUNC.Exp, scale=1.0 / math.sqrt(DK)
@@ -301,7 +319,7 @@ def tile_crossattention_pa_s_kernel(tc, query, support, Wk, Wv, out):
                     start=(c == 0),
                     stop=(c == D_PASSES - 1),
                 )
-        hold_clock(16, idle_tail)
+        hold_clock(6, idle_tail)
         val_t = keep.tile([P, HALVES, DV], F32)
         nc.scalar.copy(out=val_t[:], in_=val_ps[:])
 

import math
from contextlib import ExitStack

import concourse.mybir as mybir
from concourse.masks import make_identity

F32 = mybir.dt.float32
BF16 = mybir.dt.bfloat16
U32 = mybir.dt.uint32
U8 = mybir.dt.uint8
I32 = mybir.dt.int32
FP8X4 = mybir.dt.float8_e4m3fn_x4
ALU = mybir.AluOpType
FUNC = mybir.ActivationFunctionType
AXIS = mybir.AxisListType

P = 128
PACK = 4
K_PASS = P * PACK
QUAD = 32

B, N_SUP, D, DK, DV = 2, 16, 1024, 512, 128
U = 64
V = 16
D_PASSES = D // K_PASS
KEY_CHUNKS = DK // P
VAL_CHUNK = KEY_CHUNKS
HALVES = 2
VH = V // HALVES
SUP_COLS = N_SUP * V
CHUNK_PASSES = (4, 4, 3)
LAST_CHUNK_PASSES = 6
START_PASSES = 18

FLOPS = 2 * D * (DK * (B * U + N_SUP * V) + DV * N_SUP * V) + 2 * DK * B * U * N_SUP * V


def pass_cols(c):
    return slice(c * P, (c + 1) * P)


def block_cols(h):
    return slice(h * P, (h + 1) * P)


def tile_crossattention_pa_s_kernel(tc, query, support, Wk, Wv, out):
    nc = tc.nc
    with ExitStack() as ctx:
        ctx.enter_context(tc.manual_schedule())
        const = ctx.enter_context(tc.tile_pool(name="const", bufs=1))
        keep = ctx.enter_context(tc.tile_pool(name="keep", bufs=1))
        stage = ctx.enter_context(tc.tile_pool(name="stage", bufs=KEY_CHUNKS))
        flip_psum = ctx.enter_context(tc.psum_pool(name="flip_psum", bufs=2))
        proj_psum = ctx.enter_context(tc.psum_pool(name="proj_psum", bufs=5))
        tail_psum = ctx.enter_context(tc.psum_pool(name="tail_psum", bufs=1))

        sup_raw = keep.tile([P, D_PASSES, QUAD * 2 * V], BF16)
        sup_view = support.rearrange("n (c u g r) h w -> g c n u (r h w)", c=D_PASSES, u=2, g=P // QUAD)

        def load_support(queue, g, c):
            queue.dma_start(out=sup_raw[g * QUAD : (g + 1) * QUAD, c, :], in_=sup_view[g, c])

        w_rows = keep.tile([P, KEY_CHUNKS + 1, D], BF16)
        wk_view = Wk.rearrange("(p t) d -> p t d", t=KEY_CHUNKS)

        def load_key_chunk(t):
            nc.sync.dma_start(out=w_rows[:, t, :], in_=wk_view[:, t, :])

        for g, c in ((2, 0), (3, 0), (2, 1)):
            load_support(nc.scalar, g, c)
        for g in range(2):
            load_support(nc.sync, g, 0)
        load_key_chunk(0)
        load_support(nc.sync, 0, 1)
        load_key_chunk(1)
        for g in (1, 3):
            load_support(nc.sync, g, 1)
        for t in range(2, KEY_CHUNKS):
            load_key_chunk(t)
        q_raw = keep.tile([P, D_PASSES * K_PASS], BF16)
        for i in range(B):
            nc.sync.dma_start(
                out=q_raw[:].rearrange("p (i c u f) -> p i c u f", i=B, c=D_PASSES, u=2)[:, i],
                in_=query.rearrange("i (c u p e) h w -> p i c u (e h w)", c=D_PASSES, u=2, p=P)[:, i],
            )
        nc.sync.dma_start(out=w_rows[:, VAL_CHUNK, :], in_=Wv)

        ident = const.tile([P, P], F32)
        make_identity(nc, ident[:])
        zeros = const.tile([P, K_PASS], BF16, align_bytes=64)
        idle_codes = const.tile([P, P], U32, align_bytes=64)
        idle_scales = const.tile([P, P], U8, align_bytes=64)
        nc.vector.memset(zeros[:].bitcast(I32), 0)
        nc.vector.quantize_mx(out=idle_codes[:].bitcast(FP8X4), scales=idle_scales[:], in_=zeros[:])
        idle_ps = proj_psum.tile([P, KEY_CHUNKS, P], F32, tag="proj")

        def hold_clock(n_passes, idle_ps=idle_ps):
            for i in range(n_passes):
                nc.tensor.matmul_mx(
                    out=idle_ps[:, 0, :],
                    lhsT=idle_codes[:].bitcast(FP8X4),
                    lhsT_scale=idle_scales[:],
                    rhs=idle_codes[:].bitcast(FP8X4),
                    rhs_scale=idle_scales[:],
                    start=True,
                    stop=True,
                )

        def hold_clock_plain(n_matmuls):
            for i in range(n_matmuls):
                nc.tensor.matmul(
                    out=idle_ps[:, 0, :], lhsT=zeros[:, 0:P], rhs=zeros[:, 0:P], start=True, stop=True
                )

        hold_clock(START_PASSES)
        same_pos = const.tile([P, VH], F32)
        nc.vector.tensor_reduce(
            out=same_pos[:], in_=ident[:].rearrange("p (v n) -> p v n", n=N_SUP), axis=AXIS.X, op=ALU.add
        )
        inv_sum = const.tile([P, HALVES, B, VH], F32)
        nc.vector.memset(inv_sum[:], 0.0)
        zero_col = const.tile([P, 1], F32)
        one_col = const.tile([P, 1], F32)
        nc.vector.memset(zero_col[:], 0.0)
        nc.scalar.activation(out=one_col[:], in_=zero_col[:], func=FUNC.Exp)

        w_codes = keep.tile([P, KEY_CHUNKS + 1, D_PASSES * P], U32, align_bytes=64)
        w_scales = keep.tile([P, KEY_CHUNKS + 1, D_PASSES * P], U8, align_bytes=64)
        q_codes = keep.tile([P, D_PASSES * P], U32, align_bytes=64)
        q_scales = keep.tile([P, D_PASSES * P], U8, align_bytes=64)
        s_codes = keep.tile([P, D_PASSES, SUP_COLS], U32, align_bytes=64)
        s_scales = keep.tile([P, D_PASSES, SUP_COLS], U8, align_bytes=64)
        proj_codes = keep.tile([P, (1 + HALVES) * P], U32, align_bytes=64)
        proj_scales = keep.tile([P, (1 + HALVES) * P], U8, align_bytes=64)

        def flip_weight_chunk(t):
            words = w_rows[:, t, :].bitcast(F32).rearrange("p (c u q) -> p c u q", c=D_PASSES, u=2)
            flipped = flip_psum.tile([P, D_PASSES, 2, P], F32)
            for c in range(D_PASSES):
                for u in range(2):
                    nc.tensor.transpose(flipped[:, c, u, :], words[:, c, u, :], ident[:])
            w_grouped = stage.tile([P, D_PASSES * P * PACK], BF16, align_bytes=64)
            nc.scalar.copy(
                out=w_grouped[:].bitcast(F32).rearrange("p (c r u) -> p c r u", c=D_PASSES, u=2),
                in_=flipped[:].rearrange("p c u r -> p c r u"),
            )
            return w_grouped

        def quantise_weight_chunk(t, w_grouped):
            nc.vector.quantize_mx(out=w_codes[:, t, :].bitcast(FP8X4), scales=w_scales[:, t, :], in_=w_grouped[:])

        turned = keep.tile([P, D_PASSES, QUAD * 2 * V], BF16, align_bytes=64)
        sup_grouped = keep.tile([P, D_PASSES, QUAD * 2 * V], BF16, align_bytes=64)

        def turn_support(c, copy):
            copy(
                out=turned[:, c, :].rearrange("p (w i r) -> p w r i", w=V // PACK, i=PACK),
                in_=sup_raw[:, c, :].rearrange("p (r w i) -> p w r i", w=V // PACK, i=PACK),
            )

        def transpose_support(c):
            nc.vector.transpose(sup_grouped[:, c, :].bitcast(F32), turned[:, c, :].bitcast(F32))

        def quantise_support(c):
            nc.vector.quantize_mx(
                out=s_codes[:, c, :].bitcast(FP8X4), scales=s_scales[:, c, :], in_=sup_grouped[:, c, :]
            )

        q_grouped = keep.tile([P, D_PASSES * K_PASS], BF16, align_bytes=64)

        def regroup_query(i, passes, copy):
            copy(
                out=q_grouped[:].rearrange("p (c i s j) -> p i c s j", c=D_PASSES, i=B, j=PACK)[:, i, passes],
                in_=q_raw[:].rearrange("p (i c j s) -> p i c s j", c=D_PASSES, i=B, j=PACK)[:, i, passes],
            )

        def quantise_query(c):
            nc.vector.quantize_mx(
                out=q_codes[:, pass_cols(c)].bitcast(FP8X4),
                scales=q_scales[:, pass_cols(c)],
                in_=q_grouped[:, c * K_PASS : (c + 1) * K_PASS],
            )

        def project(proj, t, codes, scales):
            for c in range(D_PASSES):
                nc.tensor.matmul_mx(
                    out=proj,
                    lhsT=w_codes[:, t, pass_cols(c)].bitcast(FP8X4),
                    lhsT_scale=w_scales[:, t, pass_cols(c)],
                    rhs=codes[c].bitcast(FP8X4),
                    rhs_scale=scales[c],
                    start=(c == 0),
                    stop=(c == D_PASSES - 1),
                )

        def round_projection(proj, copy, proj_grouped, cols, ts):
            copy(
                out=proj_grouped[:].rearrange("p (w t) -> p w t", t=PACK)[:, cols, ts],
                in_=proj[:].rearrange("p t w -> p w t"),
            )

        def quantise_projection(cols, proj_grouped):
            nc.vector.quantize_mx(
                out=proj_codes[:, cols].bitcast(FP8X4), scales=proj_scales[:, cols], in_=proj_grouped[:]
            )

        turn_support(0, nc.vector.tensor_copy)
        transpose_support(0)
        quantise_support(0)
        w_grouped = []
        for t in range(KEY_CHUNKS):
            w_grouped.append(flip_weight_chunk(t))
            if t < KEY_CHUNKS - 1:
                hold_clock_plain(CHUNK_PASSES[t])
        hold_clock(LAST_CHUNK_PASSES)
        turn_support(1, nc.vector.tensor_copy)
        quantise_weight_chunk(0, w_grouped[0])
        transpose_support(1)
        quantise_weight_chunk(1, w_grouped[1])
        quantise_support(1)
        quantise_weight_chunk(2, w_grouped[2])
        regroup_query(0, slice(0, D_PASSES), nc.vector.tensor_copy)
        quantise_weight_chunk(3, w_grouped[3])
        regroup_query(1, slice(0, 1), nc.vector.tensor_copy)
        regroup_query(1, slice(1, 2), nc.scalar.copy)
        for c in range(D_PASSES):
            quantise_query(c)

        sup_codes = [[s_codes[:, c, block_cols(h)] for c in range(D_PASSES)] for h in range(HALVES)]
        sup_scales = [[s_scales[:, c, block_cols(h)] for c in range(D_PASSES)] for h in range(HALVES)]
        early = slice(0, 2)
        late = slice(2, KEY_CHUNKS)
        key_early = proj_psum.tile([P, 2, SUP_COLS], F32, tag="proj")
        for t in range(2):
            project(
                key_early[:, t, :],
                t,
                [s_codes[:, c, :] for c in range(D_PASSES)],
                [s_scales[:, c, :] for c in range(D_PASSES)],
            )
        key_late = [proj_psum.tile([P, 2, P], F32, name="key_late%d" % h, tag="proj") for h in range(HALVES)]
        for t in range(2, KEY_CHUNKS):
            for h in range(HALVES):
                project(key_late[h][:, t - 2, :], t, sup_codes[h], sup_scales[h])
        key_grouped = keep.tile([P, SUP_COLS * PACK], BF16, align_bytes=64)
        round_projection(key_early, nc.scalar.copy, key_grouped, slice(0, SUP_COLS), early)
        round_projection(key_late[0], nc.scalar.copy, key_grouped, block_cols(0), late)
        round_projection(key_late[1], nc.vector.tensor_copy, key_grouped, block_cols(1), late)
        q_ps = [proj_psum.tile([P, 2, P], F32, name="q_ps%d" % i, tag="proj") for i in range(2)]
        for t in range(KEY_CHUNKS):
            project(
                q_ps[t // 2][:, t % 2, :],
                t,
                [q_codes[:, pass_cols(c)] for c in range(D_PASSES)],
                [q_scales[:, pass_cols(c)] for c in range(D_PASSES)],
            )
        qp_grouped = keep.tile([P, P * PACK], BF16, align_bytes=64)
        round_projection(q_ps[0], nc.vector.tensor_copy, qp_grouped, slice(0, P), early)
        round_projection(q_ps[1], nc.scalar.copy, qp_grouped, slice(0, P), late)
        quantise_projection(slice(P, (1 + HALVES) * P), key_grouped)
        quantise_projection(slice(0, P), qp_grouped)
        wv_grouped = flip_weight_chunk(VAL_CHUNK)

        idle_tail = proj_psum.tile([P, KEY_CHUNKS, P], F32, tag="proj")
        hold_clock(4, idle_tail)

        scores = [
            tail_psum.tile([P, P], F32, name="scores0", tag="chain"),
            proj_psum.tile([P, P], F32, name="scores1", tag="proj"),
        ]
        for h in range(HALVES):
            key_cols = slice((1 + h) * P, (2 + h) * P)
            nc.tensor.matmul_mx(
                out=scores[h][:],
                lhsT=proj_codes[:, 0:P].bitcast(FP8X4),
                lhsT_scale=proj_scales[:, 0:P],
                rhs=proj_codes[:, key_cols].bitcast(FP8X4),
                rhs_scale=proj_scales[:, key_cols],
                start=True,
                stop=True,
            )
        hold_clock(10, idle_tail)

        top = keep.tile([P, V], F32)
        shifted = keep.tile([P, SUP_COLS], F32)
        expd = keep.tile([P, SUP_COLS], F32)
        sums = keep.tile([P, V], F32)

        def by_position(x):
            return x.rearrange("p (v n) -> p v n", n=N_SUP)

        def positions(h):
            return slice(h * VH, (h + 1) * VH)

        for h in range(HALVES):
            nc.vector.tensor_reduce(out=top[:, positions(h)], in_=by_position(scores[h][:]), axis=AXIS.X, op=ALU.max)
        for h in range(HALVES):
            nc.vector.tensor_tensor(
                out=by_position(shifted[:, block_cols(h)]),
                in0=by_position(scores[h][:]),
                in1=top[:, positions(h)].unsqueeze(2).to_broadcast([P, VH, N_SUP]),
                op=ALU.subtract,
            )
        quantise_weight_chunk(VAL_CHUNK, wv_grouped)
        for h in range(HALVES):
            nc.scalar.activation(
                out=expd[:, block_cols(h)], in_=shifted[:, block_cols(h)], func=FUNC.Exp, scale=1.0 / math.sqrt(DK)
            )

        val_ps = flip_psum.tile([P, HALVES, DV], F32, tag="flipped")
        for h in range(HALVES):
            for c in range(D_PASSES):
                nc.tensor.matmul_mx(
                    out=val_ps[:, h, :],
                    lhsT=sup_codes[h][c].bitcast(FP8X4),
                    lhsT_scale=sup_scales[h][c],
                    rhs=w_codes[:, VAL_CHUNK, pass_cols(c)].bitcast(FP8X4),
                    rhs_scale=w_scales[:, VAL_CHUNK, pass_cols(c)],
                    start=(c == 0),
                    stop=(c == D_PASSES - 1),
                )
        hold_clock(6, idle_tail)
        val_t = keep.tile([P, HALVES, DV], F32)
        nc.scalar.copy(out=val_t[:], in_=val_ps[:])

        for h in range(HALVES):
            nc.vector.tensor_reduce(out=sums[:, positions(h)], in_=by_position(expd[:, block_cols(h)]), axis=AXIS.X, op=ALU.add)
        for h in range(HALVES):
            for b in range(B):
                own = slice(b * U, (b + 1) * U)
                nc.vector.reciprocal(out=inv_sum[own, h, b, :], in_=sums[own, positions(h)])

        result = keep.tile([P, B, V], F32)
        weights = []
        for h in range(HALVES):
            crossed = flip_psum.tile([P, B, VH], F32, tag="flipped")
            nc.tensor.matmul(
                out=crossed[:].rearrange("p b v -> p (b v)"),
                lhsT=expd[:, block_cols(h)],
                rhs=inv_sum[:, h].rearrange("p b v -> p (b v)"),
                start=True,
                stop=True,
            )
            weight = keep.tile([P, B, VH], F32, name="weight%d" % h)
            nc.vector.tensor_tensor(
                out=weight[:], in0=crossed[:], in1=same_pos[:].unsqueeze(1).to_broadcast([P, B, VH]), op=ALU.mult
            )
            weights.append(weight)
        result_ps = tail_psum.tile([P, HALVES, B, VH], F32, tag="chain")
        for h in range(HALVES):
            nc.tensor.matmul(
                out=result_ps[:, h].rearrange("p b v -> p (b v)"),
                lhsT=val_t[:, h, :],
                rhs=weights[h][:].rearrange("p b v -> p (b v)"),
                start=True,
                stop=True,
            )
        nc.vector.tensor_copy(
            out=result[:].rearrange("p b (h v) -> p b h v", h=HALVES), in_=result_ps[:].rearrange("p h b v -> p b h v")
        )
        nc.sync.dma_start(out=out.rearrange("b c v -> c b v"), in_=result[:])
